import numpy as np
import ml_dtypes


def mxq(x, axis, fmt="e4m3"):
    dtype, down = {"e4m3": (ml_dtypes.float8_e4m3fn, 7), "e5m2": (ml_dtypes.float8_e5m2, 14)}[fmt]
    v = np.moveaxis(np.asarray(x, np.float32).astype(ml_dtypes.bfloat16).astype(np.float64), axis, -1)
    blocks = v.reshape(v.shape[:-1] + (-1, 32))
    amax = np.abs(blocks).max(-1, keepdims=True)
    byte = np.maximum(np.where(amax > 0, np.frexp(amax)[1] - 1 + 127, 0) - down, 1)
    scale = np.exp2(byte - 127.0)
    codes = (blocks / scale).astype(np.float32).astype(dtype).astype(np.float64)
    return np.moveaxis((codes * scale).reshape(v.shape), -1, axis)


WIDE = False


def mx_kscale(k):
    if not WIDE:
        return np.ones(k)
    levels = np.array([10, -10, 5, -5, 0])
    a = np.random.permutation(np.resize(levels, k // 512 * 4)).reshape(k // 512, 4)
    idx = np.arange(k)
    return np.exp2(a[idx // 512, idx % 128 // 32])


BF16 = ml_dtypes.bfloat16


def bf(x):
    return np.asarray(x, np.float32).astype(BF16)


def f64(x):
    return np.asarray(x).astype(np.float64)


B, S, D1, D2, DK, OUT = 1, 1024, 512, 512, 512, 512
EPS = 1e-5


def relu(x):
    return np.maximum(x, 0.0)


def layernorm(x, gamma, beta):
    mu = x.mean(-1, keepdims=True)
    var = np.square(x - mu).mean(-1, keepdims=True)
    return (x - mu) / np.sqrt(var + EPS) * gamma + beta


def setup_inputs():
    r = np.random.standard_normal
    s, t = mx_kscale(DK), mx_kscale(OUT)
    return {"q": bf(r((B, S, DK)) * 0.55 * s), "q_hat": bf(r((B, S, DK)) * 0.3 * s),
            "W0": bf(r((OUT, DK)) / np.sqrt(DK) / s), "b0": bf(r(OUT) * 0.2),
            "W1": bf(r((OUT, DK)) / np.sqrt(DK) / s), "b1": bf(r(OUT) * 0.2),
            "W2": bf(r((OUT, DK)) / np.sqrt(DK) / s), "b2": bf(r(OUT) * 0.2),
            "W3": bf(r((OUT, DK)) / np.sqrt(DK) / s), "b3": bf(r(OUT) * 0.2),
            "gG": bf((1.0 + 0.1 * r(OUT)) * t), "betaG": bf(0.2 * r(OUT) * t),
            "gE": bf(1.0 + 0.1 * r(OUT)), "betaE": bf(0.2 * r(OUT)),
            "Wc": bf(r((OUT, OUT)) / np.sqrt(OUT) / t), "bc": bf(r(OUT) * 0.2)}


def reference(q, q_hat, W0, b0, W1, b1, W2, b2, W3, b3, gG, betaG, gE, betaE, Wc, bc):
    qq = mxq(f64(q), 2, "e4m3")
    hq = mxq(f64(q_hat), 2, "e4m3")
    a0 = (qq @ mxq(f64(W0).T, 0, "e4m3")) + f64(b0)
    a1 = (hq @ mxq(f64(W1).T, 0, "e4m3")) + f64(b1)
    a2 = (hq @ mxq(f64(W2).T, 0, "e4m3")) + f64(b2)
    a3 = (qq @ mxq(f64(W3).T, 0, "e4m3")) + f64(b3)
    g = layernorm(relu(relu(a0) + relu(a1)), f64(gG), f64(betaG))
    e = layernorm(relu(relu(a2)), f64(gE), f64(betaE))
    c = relu((mxq(g * e, 2, "e4m3") @ mxq(f64(Wc).T, 0, "e4m3")) + f64(bc))
    q_out = relu(a3)
    return q_out + c

@@ -1,0 +1,291 @@
+import concourse.mybir as mybir
+from concourse.masks import make_identity
+
+F32 = mybir.dt.float32
+BF16 = mybir.dt.bfloat16
+U32 = mybir.dt.uint32
+U8 = mybir.dt.uint8
+FP8X4 = mybir.dt.float8_e4m3fn_x4
+ALU = mybir.AluOpType
+ACT = mybir.ActivationFunctionType
+
+P = 128
+PACK = 4
+TOKENS = 1024
+WIDTH = 512
+TILES = WIDTH // P
+HALVES = TOKENS // WIDTH
+EPS = 1e-5
+
+WORD_LANES = 2
+BF16_LANES = 4
+
+FLOPS = 5 * 2 * TOKENS * WIDTH * WIDTH
+
+
+def tile_pregatingcontextualattentiongate_pb_kernel(
+    tc, q, q_hat, W0, b0, W1, b1, W2, b2, W3, b3, gG, betaG, gE, betaE, Wc, bc, out
+):
+    nc = tc.nc
+
+    token_tiles = TOKENS // P
+    q_view = q.flatten_outer_dims().rearrange("(p r) k -> p r k", r=token_tiles)
+    q_hat_view = q_hat.flatten_outer_dims().rearrange("(p r) k -> p r k", r=token_tiles)
+    out_view = out.flatten_outer_dims().rearrange("(p r) f -> p r f", r=token_tiles)
+
+    with (
+        tc.tile_pool(name="const", bufs=1) as const,
+        tc.tile_pool(name="raw", bufs=9) as raw_pool,
+        tc.tile_pool(name="grouped", bufs=3) as grouped_pool,
+        tc.tile_pool(name="operands", bufs=1) as operands,
+        tc.tile_pool(name="major", bufs=2) as major,
+        tc.tile_pool(name="work", bufs=3) as work,
+        tc.tile_pool(name="small", bufs=4) as small,
+        tc.psum_pool(name="flip_banks", bufs=2) as flip_banks,
+        tc.psum_pool(name="mx_banks", bufs=3) as mx_banks,
+        tc.psum_pool(name="turn_banks", bufs=3) as turn_banks,
+    ):
+        ident_f32 = const.tile([P, P], F32)
+        make_identity(nc, ident_f32[:])
+        ident_bf16 = const.tile([P, P], BF16)
+        make_identity(nc, ident_bf16[:])
+        minus_half = const.tile([P, 2], F32)
+        nc.vector.memset(minus_half[:], -0.5)
+
+        def load_rows(view):
+            raw = raw_pool.tile([P, TILES * WIDTH], BF16)
+            nc.sync.dma_start(out=raw[:].rearrange("p (a k) -> p a k", a=TILES), in_=view)
+            return raw
+
+        def weight_view(w):
+            return w.rearrange("(a p) k -> p a k", p=P)
+
+        def token_half(view, h):
+            return view[:, h * TILES : (h + 1) * TILES, :]
+
+        W0_raw = load_rows(weight_view(W0))
+        q_raw = [load_rows(token_half(q_view, 0))]
+        W1_raw = load_rows(weight_view(W1))
+        q_hat_raw = [load_rows(token_half(q_hat_view, 0))]
+        W2_raw = load_rows(weight_view(W2))
+        W3_raw = load_rows(weight_view(W3))
+        q_raw.append(load_rows(token_half(q_view, 1)))
+        q_hat_raw.append(load_rows(token_half(q_hat_view, 1)))
+        Wc_raw = load_rows(weight_view(Wc))
+
+        biases = [b0, b1, b2, b3, bc]
+        bias_rows = const.tile([P, P], BF16)
+        nc.vector.memset(bias_rows[:], 0.0)
+        for j, b in enumerate(biases):
+            nc.scalar.dma_start(
+                out=bias_rows[j * TILES : (j + 1) * TILES, :],
+                in_=b.rearrange("(f c) -> f c", c=P),
+            )
+        bias_flipped = flip_banks.tile([P, P], BF16, tag="flipped")
+        nc.tensor.transpose(bias_flipped[:], bias_rows[:], ident_bf16[:])
+        bias_cols = const.tile([P, P], F32)
+        nc.vector.tensor_copy(out=bias_cols[:], in_=bias_flipped[:])
+
+        def bias_col(j, f):
+            return bias_cols[:, j * TILES + f : j * TILES + f + 1]
+
+        norm_rows = const.tile([P, WIDTH], BF16)
+        nc.vector.memset(norm_rows[:], 0.0)
+        repeated = []
+        for j, v in enumerate([gG, betaG, gE, betaE]):
+            nc.gpsimd.dma_start(
+                out=norm_rows[j : j + 1, :], in_=v.rearrange("(o c) -> o c", o=1)
+            )
+        for j in range(4):
+            spread = mx_banks.tile([P, WIDTH], F32, tag="acc")
+            nc.tensor.matmul(
+                out=spread[:],
+                lhsT=ident_bf16[:, j : j + 1].to_broadcast([P, P]),
+                rhs=norm_rows[:],
+                start=True,
+                stop=True,
+            )
+            row = const.tile([P, WIDTH], F32, name="repeated%d" % j)
+            nc.scalar.copy(out=row[:], in_=spread[:])
+            repeated.append(row)
+        gG_rep, betaG_rep, gE_rep, betaE_rep = repeated
+
+        def flip_two_tiles(rows, lanes, identity, grouped, on_scalar):
+            flipped = flip_banks.tile([P, 2, lanes, P], rows.dtype, tag="flipped")
+            for a in range(2):
+                for l in range(lanes):
+                    nc.tensor.transpose(flipped[:, a, l, :], rows[:, a, l, :], identity[:])
+            side_by_side = flipped[:].rearrange("p a l r -> p a r l")
+            if on_scalar:
+                nc.scalar.copy(out=grouped, in_=side_by_side)
+            else:
+                nc.vector.tensor_copy(out=grouped, in_=side_by_side)
+
+        def new_operand(name):
+            codes = operands.tile([P, WIDTH], U32, name=name + "_codes", align_bytes=64)
+            scales = operands.tile([P, WIDTH], U8, name=name + "_scales", align_bytes=64)
+            return codes, scales
+
+        def quantise(grouped, operand):
+            codes, scales = operand
+            nc.vector.quantize_mx(out=codes[:].bitcast(FP8X4), scales=scales[:], in_=grouped[:])
+
+        def pack_input(raw, name):
+            words = raw[:].bitcast(F32).rearrange("p (a l r) -> p a l r", a=TILES, l=WORD_LANES)
+            grouped = grouped_pool.tile([P, WIDTH * PACK], BF16, align_bytes=64)
+            grouped_words = grouped[:].bitcast(F32).rearrange(
+                "p (a r l) -> p a r l", a=TILES, l=WORD_LANES
+            )
+            for pair in range(TILES // 2):
+                two = slice(2 * pair, 2 * pair + 2)
+                flip_two_tiles(
+                    words[:, two], WORD_LANES, ident_f32, grouped_words[:, two], pair == 0
+                )
+            operand = new_operand(name)
+            quantise(grouped, operand)
+            return operand
+
+        def mx_matmul(weights, f, tokens):
+            w_codes, w_scales = weights
+            t_codes, t_scales = tokens
+            cols = slice(f * P, (f + 1) * P)
+            acc = mx_banks.tile([P, WIDTH], F32, tag="acc")
+            nc.tensor.matmul_mx(
+                out=acc[:],
+                lhsT=w_codes[:, cols].bitcast(FP8X4),
+                lhsT_scale=w_scales[:, cols],
+                rhs=t_codes[:].bitcast(FP8X4),
+                rhs_scale=t_scales[:],
+                start=True,
+                stop=True,
+            )
+            return acc
+
+        def relu_of(acc, j, f, result):
+            nc.scalar.activation(out=result, in_=acc[:], func=ACT.Relu, bias=bias_col(j, f), scale=1.0)
+
+        def turn(feature_major, a):
+            turned = turn_banks.tile([P, WIDTH], F32, tag="turned")
+            for f in range(TILES):
+                nc.tensor.transpose(
+                    turned[:, f * P : (f + 1) * P],
+                    feature_major[:, f, a * P : (a + 1) * P],
+                    ident_f32[:],
+                )
+            return turned
+
+        def gate_inputs(q_op, q_hat_op):
+            x = major.tile([P, TILES, WIDTH], F32, name="x")
+            y = major.tile([P, TILES, WIDTH], F32, name="y")
+            for f in range(TILES):
+                r0 = work.tile([P, WIDTH], F32)
+                relu_of(mx_matmul(W0_op, f, q_op), 0, f, r0[:])
+                r1 = work.tile([P, WIDTH], F32)
+                relu_of(mx_matmul(W1_op, f, q_hat_op), 1, f, r1[:])
+                nc.vector.tensor_tensor(out=x[:, f, :], in0=r0[:], in1=r1[:], op=ALU.add)
+                relu_of(mx_matmul(W2_op, f, q_hat_op), 2, f, y[:, f, :])
+            return x, y
+
+        def query_path(q_op):
+            r3 = major.tile([P, TILES, WIDTH], F32, name="r3")
+            for f in range(TILES):
+                relu_of(mx_matmul(W3_op, f, q_op), 3, f, r3[:, f, :])
+            return r3
+
+        def gate_of_tile(x, y, a, ge):
+            x_turned = turn(x, a)
+            y_turned = turn(y, a)
+            stats = small.tile([P, 2, 6], F32)
+            nc.vector.bn_stats(out=stats[:, 0, :], in_=x_turned[:])
+            nc.vector.bn_stats(out=stats[:, 1, :], in_=y_turned[:])
+            mean_var = small.tile([P, 2, 2], F32)
+            nc.vector.bn_aggr(out=mean_var[:, 0, :], in_=stats[:, 0, :])
+            nc.vector.bn_aggr(out=mean_var[:, 1, :], in_=stats[:, 1, :])
+            var_eps = small.tile([P, 2], F32)
+            nc.gpsimd.tensor_scalar(
+                out=var_eps[:], in0=mean_var[:, :, 1], scalar1=EPS, scalar2=None, op0=ALU.add
+            )
+            inv_std = small.tile([P, 2], F32)
+            nc.gpsimd.tensor_tensor(out=inv_std[:], in0=var_eps[:], in1=minus_half[:], op=ALU.pow)
+            x_gain = work.tile([P, WIDTH], F32)
+            nc.vector.scalar_tensor_tensor(
+                out=x_gain[:], in0=x_turned[:], scalar=mean_var[:, 0, 0:1], in1=gG_rep[:],
+                op0=ALU.subtract, op1=ALU.mult,
+            )
+            y_gain = work.tile([P, WIDTH], F32)
+            nc.vector.scalar_tensor_tensor(
+                out=y_gain[:], in0=y_turned[:], scalar=mean_var[:, 1, 0:1], in1=gE_rep[:],
+                op0=ALU.subtract, op1=ALU.mult,
+            )
+            g = work.tile([P, WIDTH], F32)
+            nc.vector.scalar_tensor_tensor(
+                out=g[:], in0=x_gain[:], scalar=inv_std[:, 0:1], in1=betaG_rep[:],
+                op0=ALU.mult, op1=ALU.add,
+            )
+            e = work.tile([P, WIDTH], F32)
+            nc.vector.scalar_tensor_tensor(
+                out=e[:], in0=y_gain[:], scalar=inv_std[:, 1:2], in1=betaE_rep[:],
+                op0=ALU.mult, op1=ALU.add,
+            )
+            nc.vector.tensor_tensor(out=ge, in0=g[:], in1=e[:], op=ALU.mult)
+
+        def gate(x, y, name):
+            grouped = grouped_pool.tile([P, WIDTH * PACK], BF16, align_bytes=64)
+            grouped_lanes = grouped[:].rearrange("p (a r l) -> p a r l", a=TILES, l=BF16_LANES)
+            for pair in range(TILES // 2):
+                ge_rows = work.tile([P, 2, WIDTH], BF16)
+                for a in range(2):
+                    gate_of_tile(x, y, 2 * pair + a, ge_rows[:, a, :])
+                flip_two_tiles(
+                    ge_rows[:].rearrange("p a (l r) -> p a l r", l=BF16_LANES),
+                    BF16_LANES,
+                    ident_bf16,
+                    grouped_lanes[:, 2 * pair : 2 * pair + 2],
+                    True,
+                )
+            operand = new_operand(name)
+            quantise(grouped, operand)
+            return operand
+
+        def finish(ge_op, r3, h):
+            total = major.tile([P, TILES, WIDTH], F32, name="total")
+            for f in range(TILES):
+                c = work.tile([P, WIDTH], F32)
+                relu_of(mx_matmul(Wc_op, f, ge_op), 4, f, c[:])
+                nc.vector.tensor_tensor(out=total[:, f, :], in0=c[:], in1=r3[:, f, :], op=ALU.add)
+            for a in range(TILES):
+                turned = turn(total, a)
+                result = work.tile([P, WIDTH], F32)
+                nc.scalar.copy(out=result[:], in_=turned[:])
+                nc.sync.dma_start(out=out_view[:, h * TILES + a, :], in_=result[:])
+
+        def pack_Wc(raw):
+            rows = raw[:].rearrange("p (a l r) -> p a l r", a=TILES, l=BF16_LANES)
+            grouped = grouped_pool.tile([P, WIDTH * PACK], BF16, align_bytes=64)
+            grouped_lanes = grouped[:].rearrange("p (a r l) -> p a r l", a=TILES, l=BF16_LANES)
+            for pair in range(TILES // 2):
+                two = slice(2 * pair, 2 * pair + 2)
+                flip_two_tiles(rows[:, two], BF16_LANES, ident_bf16, grouped_lanes[:, two], True)
+            operand = new_operand("Wc")
+            quantise(grouped, operand)
+            return operand
+
+        W0_op = pack_input(W0_raw, "W0")
+        q_op = [pack_input(q_raw[0], "q0")]
+        W1_op = pack_input(W1_raw, "W1")
+        q_hat_op = [pack_input(q_hat_raw[0], "q_hat0")]
+        W2_op = pack_input(W2_raw, "W2")
+        xy = [gate_inputs(q_op[0], q_hat_op[0])]
+
+        W3_op = pack_input(W3_raw, "W3")
+        q_op.append(pack_input(q_raw[1], "q1"))
+        q_hat_op.append(pack_input(q_hat_raw[1], "q_hat1"))
+        Wc_op = pack_Wc(Wc_raw)
+
+        for h in range(HALVES):
+            x, y = xy[h]
+            ge_op = gate(x, y, "ge%d" % h)
+            if h + 1 < HALVES:
+                xy.append(gate_inputs(q_op[h + 1], q_hat_op[h + 1]))
+            r3 = query_path(q_op[h])
+            finish(ge_op, r3, h)

@@ -14,7 +14,8 @@ PACK = 4
 TOKENS = 1024
 WIDTH = 512
 TILES = WIDTH // P
-HALVES = TOKENS // WIDTH
+PAIR = 2 * P
+PAIRS = TOKENS // PAIR
 EPS = 1e-5
 
 WORD_LANES = 2
@@ -35,15 +36,16 @@ def tile_pregatingcontextualattentiongate_pb_kernel(
 
     with (
         tc.tile_pool(name="const", bufs=1) as const,
-        tc.tile_pool(name="raw", bufs=9) as raw_pool,
-        tc.tile_pool(name="grouped", bufs=3) as grouped_pool,
+        tc.tile_pool(name="raw", bufs=1) as raw_pool,
+        tc.tile_pool(name="grouped", bufs=1) as grouped_pool,
         tc.tile_pool(name="operands", bufs=1) as operands,
         tc.tile_pool(name="major", bufs=2) as major,
-        tc.tile_pool(name="work", bufs=3) as work,
+        tc.tile_pool(name="work", bufs=2) as work,
         tc.tile_pool(name="small", bufs=4) as small,
         tc.psum_pool(name="flip_banks", bufs=2) as flip_banks,
-        tc.psum_pool(name="mx_banks", bufs=3) as mx_banks,
-        tc.psum_pool(name="turn_banks", bufs=3) as turn_banks,
+        tc.psum_pool(name="mx_banks", bufs=2) as mx_banks,
+        tc.psum_pool(name="norm_banks", bufs=4) as norm_banks,
+        tc.manual_schedule(),
     ):
         ident_f32 = const.tile([P, P], F32)
         make_identity(nc, ident_f32[:])
@@ -51,51 +53,224 @@ def tile_pregatingcontextualattentiongate_pb_kernel(
         make_identity(nc, ident_bf16[:])
         minus_half = const.tile([P, 2], F32)
         nc.vector.memset(minus_half[:], -0.5)
-
-        def load_rows(view):
-            raw = raw_pool.tile([P, TILES * WIDTH], BF16)
-            nc.sync.dma_start(out=raw[:].rearrange("p (a k) -> p a k", a=TILES), in_=view)
-            return raw
-
-        def weight_view(w):
-            return w.rearrange("(a p) k -> p a k", p=P)
-
-        def token_half(view, h):
-            return view[:, h * TILES : (h + 1) * TILES, :]
-
-        W0_raw = load_rows(weight_view(W0))
-        q_raw = [load_rows(token_half(q_view, 0))]
-        W1_raw = load_rows(weight_view(W1))
-        q_hat_raw = [load_rows(token_half(q_hat_view, 0))]
-        W2_raw = load_rows(weight_view(W2))
-        W3_raw = load_rows(weight_view(W3))
-        q_raw.append(load_rows(token_half(q_view, 1)))
-        q_hat_raw.append(load_rows(token_half(q_hat_view, 1)))
-        Wc_raw = load_rows(weight_view(Wc))
-
-        biases = [b0, b1, b2, b3, bc]
         bias_rows = const.tile([P, P], BF16)
         nc.vector.memset(bias_rows[:], 0.0)
-        for j, b in enumerate(biases):
+        norm_rows = const.tile([P, WIDTH], BF16)
+        nc.vector.memset(norm_rows[:], 0.0)
+
+        raw_of = {}
+
+        def load_rows(name, view):
+            tiles = view.shape[1]
+            raw = raw_pool.tile([P, tiles * WIDTH], BF16, name="raw_" + name)
+            nc.sync.dma_start(out=raw[:].rearrange("p (a k) -> p a k", a=tiles), in_=view)
+            raw_of[name] = raw
+
+        def load_weight(name, w):
+            load_rows(name, w.rearrange("(a p) k -> p a k", p=P))
+
+        def load_tokens(pair):
+            two = slice(2 * pair, 2 * pair + 2)
+            load_rows("q%d" % pair, q_view[:, two, :])
+            load_rows("q_hat%d" % pair, q_hat_view[:, two, :])
+
+        load_weight("W0", W0)
+        load_tokens(0)
+        for j, b in enumerate([b0, b1, b2, b3, bc]):
             nc.scalar.dma_start(
                 out=bias_rows[j * TILES : (j + 1) * TILES, :],
                 in_=b.rearrange("(f c) -> f c", c=P),
             )
-        bias_flipped = flip_banks.tile([P, P], BF16, tag="flipped")
+        for j, v in enumerate([gG, gE, betaG, betaE]):
+            nc.scalar.dma_start(
+                out=norm_rows[j : j + 1, :], in_=v.rearrange("(o c) -> o c", o=1)
+            )
+        load_weight("W1", W1)
+        load_weight("W2", W2)
+        load_tokens(1)
+        load_weight("W3", W3)
+        load_weight("Wc", Wc)
+        load_tokens(2)
+        load_tokens(3)
+
+        bias_flipped = flip_banks.tile([P, P], BF16, tag="bank")
         nc.tensor.transpose(bias_flipped[:], bias_rows[:], ident_bf16[:])
         bias_cols = const.tile([P, P], F32)
         nc.vector.tensor_copy(out=bias_cols[:], in_=bias_flipped[:])
 
-        def bias_col(j, f):
-            return bias_cols[:, j * TILES + f : j * TILES + f + 1]
+        def flip_two_tiles(rows, lanes, grouped, on_scalar):
+            identity = ident_f32 if lanes == WORD_LANES else ident_bf16
+            flipped = flip_banks.tile([P, 2, lanes, P], rows.dtype, tag="bank")
+            for a in range(2):
+                for l in range(lanes):
+                    nc.tensor.transpose(flipped[:, a, l, :], rows[:, a, l, :], identity[:])
+            side_by_side = flipped[:].rearrange("p a l r -> p a r l")
+            if on_scalar:
+                nc.scalar.copy(out=grouped, in_=side_by_side)
+            else:
+                nc.vector.tensor_copy(out=grouped, in_=side_by_side)
 
-        norm_rows = const.tile([P, WIDTH], BF16)
-        nc.vector.memset(norm_rows[:], 0.0)
-        repeated = []
-        for j, v in enumerate([gG, betaG, gE, betaE]):
-            nc.gpsimd.dma_start(
-                out=norm_rows[j : j + 1, :], in_=v.rearrange("(o c) -> o c", o=1)
+        def quantise(grouped, name):
+            columns = grouped.shape[1] // PACK
+            codes = operands.tile([P, columns], U32, name=name + "_codes", align_bytes=64)
+            scales = operands.tile([P, columns], U8, name=name + "_scales", align_bytes=64)
+            nc.vector.quantize_mx(out=codes[:].bitcast(FP8X4), scales=scales[:], in_=grouped[:])
+            return codes, scales
+
+        flipped_rows, packed = {}, {}
+
+        def flip_rows(name, lanes=WORD_LANES):
+            raw = raw_of[name]
+            tiles = raw.shape[1] // WIDTH
+            grouped = grouped_pool.tile(
+                [P, tiles * P * PACK], BF16, name="grouped_" + name, align_bytes=64
             )
+            source, target = raw[:], grouped[:]
+            if lanes == WORD_LANES:
+                source, target = source.bitcast(F32), target.bitcast(F32)
+            rows = source.rearrange("p (a l r) -> p a l r", a=tiles, l=lanes)
+            side_by_side = target.rearrange("p (a r l) -> p a r l", a=tiles, l=lanes)
+            for i in range(tiles // 2):
+                two = slice(2 * i, 2 * i + 2)
+                flip_two_tiles(rows[:, two], lanes, side_by_side[:, two], i == 0)
+            flipped_rows[name] = grouped
+
+        def operand(name):
+            if name not in flipped_rows:
+                flip_rows(name)
+            if name not in packed:
+                packed[name] = quantise(flipped_rows[name], name)
+            return packed[name]
+
+        def relu_matmul(weights, tokens, j, name):
+            w_codes, w_scales = weights
+            t_codes, t_scales = tokens
+            result = major.tile([P, TILES, PAIR], F32, name=name)
+            for half in range(TILES // 2):
+                acc = mx_banks.tile([P, 2, PAIR], F32, tag="acc")
+                for i in range(2):
+                    features = slice((2 * half + i) * P, (2 * half + i + 1) * P)
+                    nc.tensor.matmul_mx(
+                        out=acc[:, i, :],
+                        lhsT=w_codes[:, features].bitcast(FP8X4),
+                        lhsT_scale=w_scales[:, features],
+                        rhs=t_codes[:].bitcast(FP8X4),
+                        rhs_scale=t_scales[:],
+                        start=True,
+                        stop=True,
+                    )
+                for i in range(2):
+                    f = 2 * half + i
+                    nc.scalar.activation(
+                        out=result[:, f, :],
+                        in_=acc[:, i, :],
+                        func=ACT.Relu,
+                        bias=bias_cols[:, j * TILES + f : j * TILES + f + 1],
+                        scale=1.0,
+                    )
+            return result
+
+        def turn_sum(banks, terms, a):
+            turned = banks.tile([P, WIDTH], F32, tag="bank")
+            for f in range(TILES):
+                for i, term in enumerate(terms):
+                    nc.tensor.matmul(
+                        out=turned[:, f * P : (f + 1) * P],
+                        lhsT=term[:, f, a * P : (a + 1) * P],
+                        rhs=ident_f32[:],
+                        is_transpose=True,
+                        start=(i == 0),
+                        stop=(i == len(terms) - 1),
+                    )
+            return turned
+
+        relus, turned_xy, centred, ge_grouped, last_terms = {}, {}, {}, {}, {}
+
+        def flip_tokens(pair):
+            flip_rows("q%d" % pair)
+            flip_rows("q_hat%d" % pair)
+
+        def first_layer(pair):
+            r0 = relu_matmul(operand("W0"), operand("q%d" % pair), 0, "r0")
+            r1 = relu_matmul(operand("W1"), operand("q_hat%d" % pair), 1, "r1")
+            y = relu_matmul(operand("W2"), operand("q_hat%d" % pair), 2, "y")
+            relus[pair] = (r0, r1, y)
+
+        def turn_xy(pair):
+            r0, r1, y = relus[pair]
+            turned_xy[pair] = [
+                (turn_sum(norm_banks, [r0, r1], a), turn_sum(norm_banks, [y], a)) for a in range(2)
+            ]
+
+        def norms_first(pair):
+            centred[pair] = []
+            for x_turned, y_turned in turned_xy[pair]:
+                stats = small.tile([P, 2, 6], F32)
+                nc.vector.bn_stats(out=stats[:, 0, :], in_=x_turned[:])
+                nc.vector.bn_stats(out=stats[:, 1, :], in_=y_turned[:])
+                mean_var = small.tile([P, 2, 2], F32)
+                nc.vector.bn_aggr(out=mean_var[:, 0, :], in_=stats[:, 0, :])
+                nc.vector.bn_aggr(out=mean_var[:, 1, :], in_=stats[:, 1, :])
+                var_eps = small.tile([P, 2], F32)
+                nc.gpsimd.tensor_scalar(
+                    out=var_eps[:], in0=mean_var[:, :, 1], scalar1=EPS, scalar2=None, op0=ALU.add
+                )
+                inv_std = small.tile([P, 2], F32)
+                nc.gpsimd.tensor_tensor(
+                    out=inv_std[:], in0=var_eps[:], in1=minus_half[:], op=ALU.pow
+                )
+                x_gain = work.tile([P, WIDTH], F32)
+                nc.vector.scalar_tensor_tensor(
+                    out=x_gain[:], in0=x_turned[:], scalar=mean_var[:, 0, 0:1], in1=gG_rep[:],
+                    op0=ALU.subtract, op1=ALU.mult,
+                )
+                y_gain = work.tile([P, WIDTH], F32)
+                nc.vector.scalar_tensor_tensor(
+                    out=y_gain[:], in0=y_turned[:], scalar=mean_var[:, 1, 0:1], in1=gE_rep[:],
+                    op0=ALU.subtract, op1=ALU.mult,
+                )
+                centred[pair].append((x_gain, y_gain, inv_std))
+
+        def norms_second(pair):
+            ge_rows = work.tile([P, 2, WIDTH], BF16)
+            for a, (x_gain, y_gain, inv_std) in enumerate(centred[pair]):
+                g = work.tile([P, WIDTH], F32)
+                nc.vector.scalar_tensor_tensor(
+                    out=g[:], in0=x_gain[:], scalar=inv_std[:, 0:1], in1=betaG_rep[:],
+                    op0=ALU.mult, op1=ALU.add,
+                )
+                e = work.tile([P, WIDTH], F32)
+                nc.vector.scalar_tensor_tensor(
+                    out=e[:], in0=y_gain[:], scalar=inv_std[:, 1:2], in1=betaE_rep[:],
+                    op0=ALU.mult, op1=ALU.add,
+                )
+                nc.vector.tensor_tensor(out=ge_rows[:, a, :], in0=g[:], in1=e[:], op=ALU.mult)
+            grouped = work.tile([P, PAIR * PACK], BF16, name="ge_grouped", align_bytes=64)
+            flip_two_tiles(
+                ge_rows[:].rearrange("p a (l r) -> p a l r", l=BF16_LANES),
+                BF16_LANES,
+                grouped[:].rearrange("p (a r l) -> p a r l", a=2, l=BF16_LANES),
+                True,
+            )
+            ge_grouped[pair] = grouped
+
+        def second_layer(pair):
+            ge_op = quantise(ge_grouped[pair], "ge%d" % pair)
+            r3 = relu_matmul(operand("W3"), operand("q%d" % pair), 3, "r3")
+            c = relu_matmul(operand("Wc"), ge_op, 4, "c")
+            last_terms[pair] = [r3, c]
+
+        def store(pair):
+            for a in range(2):
+                turned = turn_sum(flip_banks, last_terms[pair], a)
+                result = work.tile([P, WIDTH], F32)
+                nc.scalar.copy(out=result[:], in_=turned[:])
+                nc.sync.dma_start(out=out_view[:, 2 * pair + a, :], in_=result[:])
+
+        first_layer(0)
+        turn_xy(0)
+
+        repeated = []
         for j in range(4):
             spread = mx_banks.tile([P, WIDTH], F32, tag="acc")
             nc.tensor.matmul(
@@ -108,184 +283,30 @@ def tile_pregatingcontextualattentiongate_pb_kernel(
             row = const.tile([P, WIDTH], F32, name="repeated%d" % j)
             nc.scalar.copy(out=row[:], in_=spread[:])
             repeated.append(row)
-        gG_rep, betaG_rep, gE_rep, betaE_rep = repeated
+        gG_rep, gE_rep, betaG_rep, betaE_rep = repeated
 
-        def flip_two_tiles(rows, lanes, identity, grouped, on_scalar):
-            flipped = flip_banks.tile([P, 2, lanes, P], rows.dtype, tag="flipped")
-            for a in range(2):
-                for l in range(lanes):
-                    nc.tensor.transpose(flipped[:, a, l, :], rows[:, a, l, :], identity[:])
-            side_by_side = flipped[:].rearrange("p a l r -> p a r l")
-            if on_scalar:
-                nc.scalar.copy(out=grouped, in_=side_by_side)
-            else:
-                nc.vector.tensor_copy(out=grouped, in_=side_by_side)
+        norms_first(0)
+        flip_tokens(1)
+        flip_rows("W3")
+        flip_rows("Wc", BF16_LANES)
+        flip_tokens(2)
+        first_layer(1)
 
-        def new_operand(name):
-            codes = operands.tile([P, WIDTH], U32, name=name + "_codes", align_bytes=64)
-            scales = operands.tile([P, WIDTH], U8, name=name + "_scales", align_bytes=64)
-            return codes, scales
+        def exists(pair):
+            return 0 <= pair < PAIRS
 
-        def quantise(grouped, operand):
-            codes, scales = operand
-            nc.vector.quantize_mx(out=codes[:].bitcast(FP8X4), scales=scales[:], in_=grouped[:])
-
-        def pack_input(raw, name):
-            words = raw[:].bitcast(F32).rearrange("p (a l r) -> p a l r", a=TILES, l=WORD_LANES)
-            grouped = grouped_pool.tile([P, WIDTH * PACK], BF16, align_bytes=64)
-            grouped_words = grouped[:].bitcast(F32).rearrange(
-                "p (a r l) -> p a r l", a=TILES, l=WORD_LANES
-            )
-            for pair in range(TILES // 2):
-                two = slice(2 * pair, 2 * pair + 2)
-                flip_two_tiles(
-                    words[:, two], WORD_LANES, ident_f32, grouped_words[:, two], pair == 0
-                )
-            operand = new_operand(name)
-            quantise(grouped, operand)
-            return operand
-
-        def mx_matmul(weights, f, tokens):
-            w_codes, w_scales = weights
-            t_codes, t_scales = tokens
-            cols = slice(f * P, (f + 1) * P)
-            acc = mx_banks.tile([P, WIDTH], F32, tag="acc")
-            nc.tensor.matmul_mx(
-                out=acc[:],
-                lhsT=w_codes[:, cols].bitcast(FP8X4),
-                lhsT_scale=w_scales[:, cols],
-                rhs=t_codes[:].bitcast(FP8X4),
-                rhs_scale=t_scales[:],
-                start=True,
-                stop=True,
-            )
-            return acc
-
-        def relu_of(acc, j, f, result):
-            nc.scalar.activation(out=result, in_=acc[:], func=ACT.Relu, bias=bias_col(j, f), scale=1.0)
-
-        def turn(feature_major, a):
-            turned = turn_banks.tile([P, WIDTH], F32, tag="turned")
-            for f in range(TILES):
-                nc.tensor.transpose(
-                    turned[:, f * P : (f + 1) * P],
-                    feature_major[:, f, a * P : (a + 1) * P],
-                    ident_f32[:],
-                )
-            return turned
-
-        def gate_inputs(q_op, q_hat_op):
-            x = major.tile([P, TILES, WIDTH], F32, name="x")
-            y = major.tile([P, TILES, WIDTH], F32, name="y")
-            for f in range(TILES):
-                r0 = work.tile([P, WIDTH], F32)
-                relu_of(mx_matmul(W0_op, f, q_op), 0, f, r0[:])
-                r1 = work.tile([P, WIDTH], F32)
-                relu_of(mx_matmul(W1_op, f, q_hat_op), 1, f, r1[:])
-                nc.vector.tensor_tensor(out=x[:, f, :], in0=r0[:], in1=r1[:], op=ALU.add)
-                relu_of(mx_matmul(W2_op, f, q_hat_op), 2, f, y[:, f, :])
-            return x, y
-
-        def query_path(q_op):
-            r3 = major.tile([P, TILES, WIDTH], F32, name="r3")
-            for f in range(TILES):
-                relu_of(mx_matmul(W3_op, f, q_op), 3, f, r3[:, f, :])
-            return r3
-
-        def gate_of_tile(x, y, a, ge):
-            x_turned = turn(x, a)
-            y_turned = turn(y, a)
-            stats = small.tile([P, 2, 6], F32)
-            nc.vector.bn_stats(out=stats[:, 0, :], in_=x_turned[:])
-            nc.vector.bn_stats(out=stats[:, 1, :], in_=y_turned[:])
-            mean_var = small.tile([P, 2, 2], F32)
-            nc.vector.bn_aggr(out=mean_var[:, 0, :], in_=stats[:, 0, :])
-            nc.vector.bn_aggr(out=mean_var[:, 1, :], in_=stats[:, 1, :])
-            var_eps = small.tile([P, 2], F32)
-            nc.gpsimd.tensor_scalar(
-                out=var_eps[:], in0=mean_var[:, :, 1], scalar1=EPS, scalar2=None, op0=ALU.add
-            )
-            inv_std = small.tile([P, 2], F32)
-            nc.gpsimd.tensor_tensor(out=inv_std[:], in0=var_eps[:], in1=minus_half[:], op=ALU.pow)
-            x_gain = work.tile([P, WIDTH], F32)
-            nc.vector.scalar_tensor_tensor(
-                out=x_gain[:], in0=x_turned[:], scalar=mean_var[:, 0, 0:1], in1=gG_rep[:],
-                op0=ALU.subtract, op1=ALU.mult,
-            )
-            y_gain = work.tile([P, WIDTH], F32)
-            nc.vector.scalar_tensor_tensor(
-                out=y_gain[:], in0=y_turned[:], scalar=mean_var[:, 1, 0:1], in1=gE_rep[:],
-                op0=ALU.subtract, op1=ALU.mult,
-            )
-            g = work.tile([P, WIDTH], F32)
-            nc.vector.scalar_tensor_tensor(
-                out=g[:], in0=x_gain[:], scalar=inv_std[:, 0:1], in1=betaG_rep[:],
-                op0=ALU.mult, op1=ALU.add,
-            )
-            e = work.tile([P, WIDTH], F32)
-            nc.vector.scalar_tensor_tensor(
-                out=e[:], in0=y_gain[:], scalar=inv_std[:, 1:2], in1=betaE_rep[:],
-                op0=ALU.mult, op1=ALU.add,
-            )
-            nc.vector.tensor_tensor(out=ge, in0=g[:], in1=e[:], op=ALU.mult)
-
-        def gate(x, y, name):
-            grouped = grouped_pool.tile([P, WIDTH * PACK], BF16, align_bytes=64)
-            grouped_lanes = grouped[:].rearrange("p (a r l) -> p a r l", a=TILES, l=BF16_LANES)
-            for pair in range(TILES // 2):
-                ge_rows = work.tile([P, 2, WIDTH], BF16)
-                for a in range(2):
-                    gate_of_tile(x, y, 2 * pair + a, ge_rows[:, a, :])
-                flip_two_tiles(
-                    ge_rows[:].rearrange("p a (l r) -> p a l r", l=BF16_LANES),
-                    BF16_LANES,
-                    ident_bf16,
-                    grouped_lanes[:, 2 * pair : 2 * pair + 2],
-                    True,
-                )
-            operand = new_operand(name)
-            quantise(grouped, operand)
-            return operand
-
-        def finish(ge_op, r3, h):
-            total = major.tile([P, TILES, WIDTH], F32, name="total")
-            for f in range(TILES):
-                c = work.tile([P, WIDTH], F32)
-                relu_of(mx_matmul(Wc_op, f, ge_op), 4, f, c[:])
-                nc.vector.tensor_tensor(out=total[:, f, :], in0=c[:], in1=r3[:, f, :], op=ALU.add)
-            for a in range(TILES):
-                turned = turn(total, a)
-                result = work.tile([P, WIDTH], F32)
-                nc.scalar.copy(out=result[:], in_=turned[:])
-                nc.sync.dma_start(out=out_view[:, h * TILES + a, :], in_=result[:])
-
-        def pack_Wc(raw):
-            rows = raw[:].rearrange("p (a l r) -> p a l r", a=TILES, l=BF16_LANES)
-            grouped = grouped_pool.tile([P, WIDTH * PACK], BF16, align_bytes=64)
-            grouped_lanes = grouped[:].rearrange("p (a r l) -> p a r l", a=TILES, l=BF16_LANES)
-            for pair in range(TILES // 2):
-                two = slice(2 * pair, 2 * pair + 2)
-                flip_two_tiles(rows[:, two], BF16_LANES, ident_bf16, grouped_lanes[:, two], True)
-            operand = new_operand("Wc")
-            quantise(grouped, operand)
-            return operand
-
-        W0_op = pack_input(W0_raw, "W0")
-        q_op = [pack_input(q_raw[0], "q0")]
-        W1_op = pack_input(W1_raw, "W1")
-        q_hat_op = [pack_input(q_hat_raw[0], "q_hat0")]
-        W2_op = pack_input(W2_raw, "W2")
-        xy = [gate_inputs(q_op[0], q_hat_op[0])]
-
-        W3_op = pack_input(W3_raw, "W3")
-        q_op.append(pack_input(q_raw[1], "q1"))
-        q_hat_op.append(pack_input(q_hat_raw[1], "q_hat1"))
-        Wc_op = pack_Wc(Wc_raw)
-
-        for h in range(HALVES):
-            x, y = xy[h]
-            ge_op = gate(x, y, "ge%d" % h)
-            if h + 1 < HALVES:
-                xy.append(gate_inputs(q_op[h + 1], q_hat_op[h + 1]))
-            r3 = query_path(q_op[h])
-            finish(ge_op, r3, h)
+        for s in range(PAIRS + 2):
+            if exists(s - 1):
+                second_layer(s - 1)
+            if exists(s - 2):
+                store(s - 2)
+            if exists(s + 1):
+                turn_xy(s + 1)
+            if exists(s + 2):
+                first_layer(s + 2)
+            if exists(s + 3):
+                flip_tokens(s + 3)
+            if exists(s):
+                norms_second(s)
+            if exists(s + 1):
+                norms_first(s + 1)

@@ -45,7 +45,6 @@ def tile_pregatingcontextualattentiongate_pb_kernel(
         tc.psum_pool(name="flip_banks", bufs=2) as flip_banks,
         tc.psum_pool(name="mx_banks", bufs=2) as mx_banks,
         tc.psum_pool(name="norm_banks", bufs=4) as norm_banks,
-        tc.manual_schedule(),
     ):
         ident_f32 = const.tile([P, P], F32)
         make_identity(nc, ident_f32[:])
@@ -93,11 +92,6 @@ def tile_pregatingcontextualattentiongate_pb_kernel(
         load_tokens(2)
         load_tokens(3)
 
-        bias_flipped = flip_banks.tile([P, P], BF16, tag="bank")
-        nc.tensor.transpose(bias_flipped[:], bias_rows[:], ident_bf16[:])
-        bias_cols = const.tile([P, P], F32)
-        nc.vector.tensor_copy(out=bias_cols[:], in_=bias_flipped[:])
-
         def flip_two_tiles(rows, lanes, grouped, on_scalar):
             identity = ident_f32 if lanes == WORD_LANES else ident_bf16
             flipped = flip_banks.tile([P, 2, lanes, P], rows.dtype, tag="bank")
@@ -119,7 +113,7 @@ def tile_pregatingcontextualattentiongate_pb_kernel(
 
         flipped_rows, packed = {}, {}
 
-        def flip_rows(name, lanes=WORD_LANES):
+        def flip_rows(name, lanes=WORD_LANES, vector_helps=True):
             raw = raw_of[name]
             tiles = raw.shape[1] // WIDTH
             grouped = grouped_pool.tile(
@@ -132,7 +126,7 @@ def tile_pregatingcontextualattentiongate_pb_kernel(
             side_by_side = target.rearrange("p (a r l) -> p a r l", a=tiles, l=lanes)
             for i in range(tiles // 2):
                 two = slice(2 * i, 2 * i + 2)
-                flip_two_tiles(rows[:, two], lanes, side_by_side[:, two], i == 0)
+                flip_two_tiles(rows[:, two], lanes, side_by_side[:, two], i == 0 or not vector_helps)
             flipped_rows[name] = grouped
 
         def operand(name):
@@ -184,56 +178,57 @@ def tile_pregatingcontextualattentiongate_pb_kernel(
                     )
             return turned
 
-        relus, turned_xy, centred, ge_grouped, last_terms = {}, {}, {}, {}, {}
+        terms = {}
+        turned_xy = {}
+        ge_of = {}
+        centred = {}
 
         def flip_tokens(pair):
             flip_rows("q%d" % pair)
             flip_rows("q_hat%d" % pair)
 
-        def first_layer(pair):
-            r0 = relu_matmul(operand("W0"), operand("q%d" % pair), 0, "r0")
-            r1 = relu_matmul(operand("W1"), operand("q_hat%d" % pair), 1, "r1")
-            y = relu_matmul(operand("W2"), operand("q_hat%d" % pair), 2, "y")
-            relus[pair] = (r0, r1, y)
+        def relu_term(name, weight, tokens, j, pair):
+            terms[name, pair] = relu_matmul(
+                operand(weight), operand("%s%d" % (tokens, pair)), j, name
+            )
 
-        def turn_xy(pair):
-            r0, r1, y = relus[pair]
-            turned_xy[pair] = [
-                (turn_sum(norm_banks, [r0, r1], a), turn_sum(norm_banks, [y], a)) for a in range(2)
-            ]
+        def turn_tile(pair, a):
+            x_turned = turn_sum(norm_banks, [terms["r0", pair], terms["r1", pair]], a)
+            y_turned = turn_sum(norm_banks, [terms["y", pair]], a)
+            turned_xy[pair, a] = (x_turned, y_turned)
 
-        def norms_first(pair):
-            centred[pair] = []
-            for x_turned, y_turned in turned_xy[pair]:
-                stats = small.tile([P, 2, 6], F32)
-                nc.vector.bn_stats(out=stats[:, 0, :], in_=x_turned[:])
-                nc.vector.bn_stats(out=stats[:, 1, :], in_=y_turned[:])
-                mean_var = small.tile([P, 2, 2], F32)
-                nc.vector.bn_aggr(out=mean_var[:, 0, :], in_=stats[:, 0, :])
-                nc.vector.bn_aggr(out=mean_var[:, 1, :], in_=stats[:, 1, :])
-                var_eps = small.tile([P, 2], F32)
-                nc.gpsimd.tensor_scalar(
-                    out=var_eps[:], in0=mean_var[:, :, 1], scalar1=EPS, scalar2=None, op0=ALU.add
-                )
-                inv_std = small.tile([P, 2], F32)
-                nc.gpsimd.tensor_tensor(
-                    out=inv_std[:], in0=var_eps[:], in1=minus_half[:], op=ALU.pow
-                )
-                x_gain = work.tile([P, WIDTH], F32)
-                nc.vector.scalar_tensor_tensor(
-                    out=x_gain[:], in0=x_turned[:], scalar=mean_var[:, 0, 0:1], in1=gG_rep[:],
-                    op0=ALU.subtract, op1=ALU.mult,
-                )
-                y_gain = work.tile([P, WIDTH], F32)
-                nc.vector.scalar_tensor_tensor(
-                    out=y_gain[:], in0=y_turned[:], scalar=mean_var[:, 1, 0:1], in1=gE_rep[:],
-                    op0=ALU.subtract, op1=ALU.mult,
-                )
-                centred[pair].append((x_gain, y_gain, inv_std))
+        def norms_first(pair, a):
+            x_turned, y_turned = turned_xy[pair, a]
+            stats = small.tile([P, 2, 6], F32)
+            nc.vector.bn_stats(out=stats[:, 0, :], in_=x_turned[:])
+            nc.vector.bn_stats(out=stats[:, 1, :], in_=y_turned[:])
+            mean_var = small.tile([P, 2, 2], F32)
+            nc.vector.bn_aggr(out=mean_var[:, 0, :], in_=stats[:, 0, :])
+            nc.vector.bn_aggr(out=mean_var[:, 1, :], in_=stats[:, 1, :])
+            var_eps = small.tile([P, 2], F32)
+            nc.gpsimd.tensor_scalar(
+                out=var_eps[:], in0=mean_var[:, :, 1], scalar1=EPS, scalar2=None, op0=ALU.add
+            )
+            inv_std = small.tile([P, 2], F32)
+            nc.gpsimd.tensor_tensor(
+                out=inv_std[:], in0=var_eps[:], in1=minus_half[:], op=ALU.pow
+            )
+            x_gain = work.tile([P, WIDTH], F32)
+            nc.vector.scalar_tensor_tensor(
+                out=x_gain[:], in0=x_turned[:], scalar=mean_var[:, 0, 0:1], in1=gG_rep[:],
+                op0=ALU.subtract, op1=ALU.mult,
+            )
+            y_gain = work.tile([P, WIDTH], F32)
+            nc.vector.scalar_tensor_tensor(
+                out=y_gain[:], in0=y_turned[:], scalar=mean_var[:, 1, 0:1], in1=gE_rep[:],
+                op0=ALU.subtract, op1=ALU.mult,
+            )
+            centred[pair, a] = (x_gain, y_gain, inv_std)
 
         def norms_second(pair):
             ge_rows = work.tile([P, 2, WIDTH], BF16)
-            for a, (x_gain, y_gain, inv_std) in enumerate(centred[pair]):
+            for a in range(2):
+                x_gain, y_gain, inv_std = centred[pair, a]
                 g = work.tile([P, WIDTH], F32)
                 nc.vector.scalar_tensor_tensor(
                     out=g[:], in0=x_gain[:], scalar=inv_std[:, 0:1], in1=betaG_rep[:],
@@ -245,6 +240,10 @@ def tile_pregatingcontextualattentiongate_pb_kernel(
                     op0=ALU.mult, op1=ALU.add,
                 )
                 nc.vector.tensor_tensor(out=ge_rows[:, a, :], in0=g[:], in1=e[:], op=ALU.mult)
+            ge_of[pair] = ge_rows
+
+        def flip_gate(pair):
+            ge_rows = ge_of[pair]
             grouped = work.tile([P, PAIR * PACK], BF16, name="ge_grouped", align_bytes=64)
             flip_two_tiles(
                 ge_rows[:].rearrange("p a (l r) -> p a l r", l=BF16_LANES),
@@ -252,23 +251,29 @@ def tile_pregatingcontextualattentiongate_pb_kernel(
                 grouped[:].rearrange("p (a r l) -> p a r l", a=2, l=BF16_LANES),
                 True,
             )
-            ge_grouped[pair] = grouped
+            flipped_rows["ge%d" % pair] = grouped
 
-        def second_layer(pair):
-            ge_op = quantise(ge_grouped[pair], "ge%d" % pair)
-            r3 = relu_matmul(operand("W3"), operand("q%d" % pair), 3, "r3")
-            c = relu_matmul(operand("Wc"), ge_op, 4, "c")
-            last_terms[pair] = [r3, c]
+        def store_tile(pair, a):
+            turned = turn_sum(flip_banks, [terms["r3", pair], terms["c", pair]], a)
+            result = work.tile([P, WIDTH], F32, bufs=4)
+            nc.scalar.copy(out=result[:], in_=turned[:])
+            nc.sync.dma_start(out=out_view[:, 2 * pair + a, :], in_=result[:])
 
-        def store(pair):
-            for a in range(2):
-                turned = turn_sum(flip_banks, last_terms[pair], a)
-                result = work.tile([P, WIDTH], F32)
-                nc.scalar.copy(out=result[:], in_=turned[:])
-                nc.sync.dma_start(out=out_view[:, 2 * pair + a, :], in_=result[:])
+        operand("W0")
+        operand("q0")
+        operand("q_hat0")
 
-        first_layer(0)
-        turn_xy(0)
+        bias_flipped = flip_banks.tile([P, P], BF16, tag="bank")
+        nc.tensor.transpose(bias_flipped[:], bias_rows[:], ident_bf16[:])
+        bias_cols = const.tile([P, P], F32)
+        nc.vector.tensor_copy(out=bias_cols[:], in_=bias_flipped[:])
+
+        operand("W1")
+        relu_term("r0", "W0", "q", 0, 0)
+        operand("W2")
+        relu_term("r1", "W1", "q_hat", 1, 0)
+        relu_term("y", "W2", "q_hat", 2, 0)
+        turn_tile(0, 0)
 
         repeated = []
         for j in range(4):
@@ -285,28 +290,46 @@ def tile_pregatingcontextualattentiongate_pb_kernel(
             repeated.append(row)
         gG_rep, gE_rep, betaG_rep, betaE_rep = repeated
 
-        norms_first(0)
+
+        turn_tile(0, 1)
         flip_tokens(1)
-        flip_rows("W3")
-        flip_rows("Wc", BF16_LANES)
+        norms_first(0, 0)
+        norms_first(0, 1)
+        relu_term("r0", "W0", "q", 0, 1)
+        relu_term("r1", "W1", "q_hat", 1, 1)
+        relu_term("y", "W2", "q_hat", 2, 1)
         flip_tokens(2)
-        first_layer(1)
+        flip_rows("W3", vector_helps=False)
+        flip_rows("Wc", BF16_LANES, vector_helps=False)
 
         def exists(pair):
             return 0 <= pair < PAIRS
 
         for s in range(PAIRS + 2):
-            if exists(s - 1):
-                second_layer(s - 1)
-            if exists(s - 2):
-                store(s - 2)
-            if exists(s + 1):
-                turn_xy(s + 1)
-            if exists(s + 2):
-                first_layer(s + 2)
-            if exists(s + 3):
-                flip_tokens(s + 3)
             if exists(s):
                 norms_second(s)
             if exists(s + 1):
-                norms_first(s + 1)
+                turn_tile(s + 1, 0)
+            if exists(s - 1):
+                relu_term("r3", "W3", "q", 3, s - 1)
+            if exists(s + 1):
+                turn_tile(s + 1, 1)
+            if exists(s - 1):
+                relu_term("c", "Wc", "ge", 4, s - 1)
+            if exists(s + 2):
+                relu_term("r0", "W0", "q", 0, s + 2)
+            if exists(s - 2):
+                store_tile(s - 2, 0)
+            if exists(s + 2):
+                relu_term("r1", "W1", "q_hat", 1, s + 2)
+            if exists(s - 2):
+                store_tile(s - 2, 1)
+            if exists(s + 2):
+                relu_term("y", "W2", "q_hat", 2, s + 2)
+            if exists(s + 3):
+                flip_tokens(s + 3)
+            if exists(s):
+                flip_gate(s)
+            if exists(s + 1):
+                norms_first(s + 1, 0)
+                norms_first(s + 1, 1)

@@ -18,9 +18,6 @@ PAIR = 2 * P
 PAIRS = TOKENS // PAIR
 EPS = 1e-5
 
-WORD_LANES = 2
-BF16_LANES = 4
-
 FLOPS = 5 * 2 * TOKENS * WIDTH * WIDTH
 
 
@@ -30,9 +27,12 @@ def tile_pregatingcontextualattentiongate_pb_kernel(
     nc = tc.nc
 
     token_tiles = TOKENS // P
-    q_view = q.flatten_outer_dims().rearrange("(p r) k -> p r k", r=token_tiles)
-    q_hat_view = q_hat.flatten_outer_dims().rearrange("(p r) k -> p r k", r=token_tiles)
+    views = {
+        "q": q.flatten_outer_dims().rearrange("(p r) k -> p r k", r=token_tiles),
+        "h": q_hat.flatten_outer_dims().rearrange("(p r) k -> p r k", r=token_tiles),
+    }
     out_view = out.flatten_outer_dims().rearrange("(p r) f -> p r f", r=token_tiles)
+    weights = {"W0": W0, "W1": W1, "W2": W2, "W3": W3, "Wc": Wc}
 
     with (
         tc.tile_pool(name="const", bufs=1) as const,
@@ -42,294 +42,402 @@ def tile_pregatingcontextualattentiongate_pb_kernel(
         tc.tile_pool(name="major", bufs=2) as major,
         tc.tile_pool(name="work", bufs=2) as work,
         tc.tile_pool(name="small", bufs=4) as small,
-        tc.psum_pool(name="flip_banks", bufs=2) as flip_banks,
-        tc.psum_pool(name="mx_banks", bufs=2) as mx_banks,
+        tc.psum_pool(name="banks", bufs=4) as banks,
         tc.psum_pool(name="norm_banks", bufs=4) as norm_banks,
+        tc.manual_schedule(),
     ):
+        bias_rows = [const.tile([P, P], BF16, name="bias_rows%d" % i) for i in range(2)]
+        for rows in bias_rows:
+            nc.vector.memset(rows[:], 0.0)
+        norm_rows = const.tile([P, WIDTH], BF16)
+        nc.vector.memset(norm_rows[:], 0.0)
+        minus_half = const.tile([P, 2], F32)
+        nc.vector.memset(minus_half[:], -0.5)
         ident_f32 = const.tile([P, P], F32)
         make_identity(nc, ident_f32[:])
         ident_bf16 = const.tile([P, P], BF16)
-        make_identity(nc, ident_bf16[:])
-        minus_half = const.tile([P, 2], F32)
-        nc.vector.memset(minus_half[:], -0.5)
-        bias_rows = const.tile([P, P], BF16)
-        nc.vector.memset(bias_rows[:], 0.0)
-        norm_rows = const.tile([P, WIDTH], BF16)
-        nc.vector.memset(norm_rows[:], 0.0)
+        nc.vector.tensor_copy(out=ident_bf16[:], in_=ident_f32[:])
 
         raw_of = {}
 
-        def load_rows(name, view):
-            tiles = view.shape[1]
-            raw = raw_pool.tile([P, tiles * WIDTH], BF16, name="raw_" + name)
-            nc.sync.dma_start(out=raw[:].rearrange("p (a k) -> p a k", a=tiles), in_=view)
-            raw_of[name] = raw
+        def load(name, view):
+            raw = raw_pool.tile([P, 2 * WIDTH], BF16, name="raw_" + name)
+            nc.sync.dma_start(out=raw[:].rearrange("p (a k) -> p a k", a=2), in_=view)
+            raw_of[name] = raw[:]
 
-        def load_weight(name, w):
-            load_rows(name, w.rearrange("(a p) k -> p a k", p=P))
+        def load_half(name, half):
+            rows = weights[name][half * PAIR : (half + 1) * PAIR, :]
+            load("%s_%d" % (name, half), rows.rearrange("(p a) k -> p a k", a=2))
 
-        def load_tokens(pair):
-            two = slice(2 * pair, 2 * pair + 2)
-            load_rows("q%d" % pair, q_view[:, two, :])
-            load_rows("q_hat%d" % pair, q_hat_view[:, two, :])
+        def load_weight(name):
+            for half in range(2):
+                load_half(name, half)
 
-        load_weight("W0", W0)
-        load_tokens(0)
-        for j, b in enumerate([b0, b1, b2, b3, bc]):
-            nc.scalar.dma_start(
-                out=bias_rows[j * TILES : (j + 1) * TILES, :],
+        def load_tokens(name, pair):
+            load("%s_%d" % (name, pair), views[name][:, 2 * pair : 2 * pair + 2, :])
+
+        def load_bias(queue, i, j, b):
+            queue.dma_start(
+                out=bias_rows[i][j * TILES : (j + 1) * TILES, :],
                 in_=b.rearrange("(f c) -> f c", c=P),
             )
+
+        load_tokens("q", 0)
+        load_weight("W0")
+        load_tokens("h", 0)
+        load_weight("W1")
+        load_bias(nc.scalar, 0, 0, b0)
+        load_bias(nc.scalar, 0, 1, b1)
+        load_weight("W2")
+        load_tokens("q", 1)
+        load_tokens("h", 1)
+        load_weight("W3")
+        load_tokens("q", 2)
+        load_tokens("h", 2)
+        load_weight("Wc")
+        load_tokens("q", 3)
+        load_tokens("h", 3)
+
+        load_bias(nc.gpsimd, 0, 2, b2)
         for j, v in enumerate([gG, gE, betaG, betaE]):
-            nc.scalar.dma_start(
+            nc.gpsimd.dma_start(
                 out=norm_rows[j : j + 1, :], in_=v.rearrange("(o c) -> o c", o=1)
             )
-        load_weight("W1", W1)
-        load_weight("W2", W2)
-        load_tokens(1)
-        load_weight("W3", W3)
-        load_weight("Wc", Wc)
-        load_tokens(2)
-        load_tokens(3)
+        load_bias(nc.gpsimd, 1, 0, b3)
+        load_bias(nc.gpsimd, 1, 1, bc)
+        table_loader = const.tile([P, 2], F32)
+        nc.scalar.activation(
+            out=table_loader[:], in_=minus_half[:], func=ACT.Relu, bias=0.0, scale=1.0
+        )
 
-        def flip_two_tiles(rows, lanes, grouped, on_scalar):
-            identity = ident_f32 if lanes == WORD_LANES else ident_bf16
-            flipped = flip_banks.tile([P, 2, lanes, P], rows.dtype, tag="bank")
-            for a in range(2):
-                for l in range(lanes):
-                    nc.tensor.transpose(flipped[:, a, l, :], rows[:, a, l, :], identity[:])
-            side_by_side = flipped[:].rearrange("p a l r -> p a r l")
-            if on_scalar:
-                nc.scalar.copy(out=grouped, in_=side_by_side)
+        packed = {}
+
+        def flip(rows, grouped, is_weight, engine, pool):
+            tiles = rows.shape[1] // WIDTH
+            flipped = pool.tile([P, tiles, 2, P], F32, tag="bank")
+            words = rows.bitcast(F32).rearrange("p (a l r) -> p a l r", a=tiles, l=2)
+            for a in range(tiles):
+                for l in range(2):
+                    nc.tensor.transpose(flipped[:, a, l, :], words[:, a, l, :], ident_f32[:])
+            target = grouped.bitcast(F32)
+            if is_weight:
+                source = flipped[:].rearrange("p a l r -> p r a l")
+                target = target.rearrange("p (r a l) -> p r a l", a=2, l=2)
             else:
-                nc.vector.tensor_copy(out=grouped, in_=side_by_side)
+                source = flipped[:].rearrange("p a l r -> p a r l")
+                target = target.rearrange("p (a r l) -> p a r l", a=tiles, l=2)
+            if engine == "scalar":
+                nc.scalar.copy(out=target, in_=source)
+            else:
+                nc.vector.tensor_copy(out=target, in_=source)
 
-        def quantise(grouped, name):
-            columns = grouped.shape[1] // PACK
+        grouped_of = {}
+
+        def flip_rows(name, engine, pool=banks):
+            grouped = grouped_pool.tile([P, PAIR * PACK], BF16, name="grouped_" + name, align_bytes=64)
+            flip(raw_of[name], grouped[:], name[0] == "W", engine, pool)
+            grouped_of[name] = grouped
+
+        def quantise(name):
+            columns = grouped_of[name].shape[1] // PACK
             codes = operands.tile([P, columns], U32, name=name + "_codes", align_bytes=64)
             scales = operands.tile([P, columns], U8, name=name + "_scales", align_bytes=64)
-            nc.vector.quantize_mx(out=codes[:].bitcast(FP8X4), scales=scales[:], in_=grouped[:])
-            return codes, scales
-
-        flipped_rows, packed = {}, {}
-
-        def flip_rows(name, lanes=WORD_LANES, vector_helps=True):
-            raw = raw_of[name]
-            tiles = raw.shape[1] // WIDTH
-            grouped = grouped_pool.tile(
-                [P, tiles * P * PACK], BF16, name="grouped_" + name, align_bytes=64
+            nc.vector.quantize_mx(
+                out=codes[:].bitcast(FP8X4), scales=scales[:], in_=grouped_of[name][:]
             )
-            source, target = raw[:], grouped[:]
-            if lanes == WORD_LANES:
-                source, target = source.bitcast(F32), target.bitcast(F32)
-            rows = source.rearrange("p (a l r) -> p a l r", a=tiles, l=lanes)
-            side_by_side = target.rearrange("p (a r l) -> p a r l", a=tiles, l=lanes)
-            for i in range(tiles // 2):
-                two = slice(2 * i, 2 * i + 2)
-                flip_two_tiles(rows[:, two], lanes, side_by_side[:, two], i == 0 or not vector_helps)
-            flipped_rows[name] = grouped
+            packed[name] = (codes, scales)
 
-        def operand(name):
-            if name not in flipped_rows:
-                flip_rows(name)
-            if name not in packed:
-                packed[name] = quantise(flipped_rows[name], name)
-            return packed[name]
+        terms = {}
 
-        def relu_matmul(weights, tokens, j, name):
-            w_codes, w_scales = weights
-            t_codes, t_scales = tokens
-            result = major.tile([P, TILES, PAIR], F32, name=name)
-            for half in range(TILES // 2):
-                acc = mx_banks.tile([P, 2, PAIR], F32, tag="acc")
-                for i in range(2):
-                    features = slice((2 * half + i) * P, (2 * half + i + 1) * P)
-                    nc.tensor.matmul_mx(
-                        out=acc[:, i, :],
-                        lhsT=w_codes[:, features].bitcast(FP8X4),
-                        lhsT_scale=w_scales[:, features],
-                        rhs=t_codes[:].bitcast(FP8X4),
-                        rhs_scale=t_scales[:],
-                        start=True,
-                        stop=True,
-                    )
-                for i in range(2):
-                    f = 2 * half + i
-                    nc.scalar.activation(
-                        out=result[:, f, :],
-                        in_=acc[:, i, :],
-                        func=ACT.Relu,
-                        bias=bias_cols[:, j * TILES + f : j * TILES + f + 1],
-                        scale=1.0,
-                    )
-            return result
+        def add_bias_relu(engine, target, source, i_bias, column):
+            bias = bias_cols[i_bias][:, column : column + 1]
+            if engine == "scalar":
+                nc.scalar.activation(out=target, in_=source, func=ACT.Relu, bias=bias, scale=1.0)
+            else:
+                nc.vector.tensor_scalar(
+                    out=target, in0=source, scalar1=bias, scalar2=0.0, op0=ALU.add, op1=ALU.max
+                )
 
-        def turn_sum(banks, terms, a):
-            turned = banks.tile([P, WIDTH], F32, tag="bank")
+        def relu_half(name, pair, half, engine):
+            weight, tokens, (i_bias, j) = {
+                "r0": ("W0", "q", (0, 0)), "r1": ("W1", "h", (0, 1)), "y": ("W2", "h", (0, 2)),
+                "r3": ("W3", "q", (1, 0)), "c": ("Wc", "ge", (1, 1)),
+            }[name]
+            w_codes, w_scales = packed["%s_%d" % (weight, half)]
+            t_codes, t_scales = packed["%s_%d" % (tokens, pair)]
+            if half == 0:
+                terms[name, pair] = major.tile([P, TILES, PAIR], F32, name=name)
+            result = terms[name, pair]
+            acc = banks.tile([P, 2, PAIR], F32, tag="bank")
+            for i in range(2):
+                features = slice(i * P, (i + 1) * P)
+                nc.tensor.matmul_mx(
+                    out=acc[:, i, :],
+                    lhsT=w_codes[:, features].bitcast(FP8X4),
+                    lhsT_scale=w_scales[:, features],
+                    rhs=t_codes[:].bitcast(FP8X4),
+                    rhs_scale=t_scales[:],
+                    start=True,
+                    stop=True,
+                )
+            for i in range(2):
+                f = 2 * half + i
+                add_bias_relu(engine, result[:, f, :], acc[:, i, :], i_bias, j * TILES + f)
+
+        def relu_term(name, pair):
+            for half in range(2):
+                relu_half(name, pair, half, "scalar")
+
+        def turn_sum(bank, parts, a):
             for f in range(TILES):
-                for i, term in enumerate(terms):
+                for i, part in enumerate(parts):
                     nc.tensor.matmul(
-                        out=turned[:, f * P : (f + 1) * P],
-                        lhsT=term[:, f, a * P : (a + 1) * P],
+                        out=bank[:, f * P : (f + 1) * P],
+                        lhsT=part[:, f, a * P : (a + 1) * P],
                         rhs=ident_f32[:],
                         is_transpose=True,
                         start=(i == 0),
-                        stop=(i == len(terms) - 1),
+                        stop=(i == len(parts) - 1),
                     )
-            return turned
 
-        terms = {}
-        turned_xy = {}
-        ge_of = {}
+        turned = {}
         centred = {}
+        normed = {}
+        ge_of = {}
 
-        def flip_tokens(pair):
-            flip_rows("q%d" % pair)
-            flip_rows("q_hat%d" % pair)
+        def turn_tile(t):
+            pair, a = divmod(t, 2)
+            x_bank = norm_banks.tile([P, WIDTH], F32, tag="bank")
+            turn_sum(x_bank, [terms["r0", pair], terms["r1", pair]], a)
+            y_bank = norm_banks.tile([P, WIDTH], F32, tag="bank")
+            turn_sum(y_bank, [terms["y", pair]], a)
+            turned[t] = (x_bank, y_bank)
 
-        def relu_term(name, weight, tokens, j, pair):
-            terms[name, pair] = relu_matmul(
-                operand(weight), operand("%s%d" % (tokens, pair)), j, name
-            )
+        def statistics(t, i, stats):
+            nc.vector.bn_stats(out=stats[:, i, :], in_=turned[t][i][:])
 
-        def turn_tile(pair, a):
-            x_turned = turn_sum(norm_banks, [terms["r0", pair], terms["r1", pair]], a)
-            y_turned = turn_sum(norm_banks, [terms["y", pair]], a)
-            turned_xy[pair, a] = (x_turned, y_turned)
-
-        def norms_first(pair, a):
-            x_turned, y_turned = turned_xy[pair, a]
-            stats = small.tile([P, 2, 6], F32)
-            nc.vector.bn_stats(out=stats[:, 0, :], in_=x_turned[:])
-            nc.vector.bn_stats(out=stats[:, 1, :], in_=y_turned[:])
-            mean_var = small.tile([P, 2, 2], F32)
-            nc.vector.bn_aggr(out=mean_var[:, 0, :], in_=stats[:, 0, :])
-            nc.vector.bn_aggr(out=mean_var[:, 1, :], in_=stats[:, 1, :])
-            var_eps = small.tile([P, 2], F32)
-            nc.gpsimd.tensor_scalar(
-                out=var_eps[:], in0=mean_var[:, :, 1], scalar1=EPS, scalar2=None, op0=ALU.add
-            )
-            inv_std = small.tile([P, 2], F32)
-            nc.gpsimd.tensor_tensor(
-                out=inv_std[:], in0=var_eps[:], in1=minus_half[:], op=ALU.pow
-            )
-            x_gain = work.tile([P, WIDTH], F32)
+        def centre(t, i, mean_var):
+            result = work.tile([P, WIDTH], F32, name="centred%d" % i)
             nc.vector.scalar_tensor_tensor(
-                out=x_gain[:], in0=x_turned[:], scalar=mean_var[:, 0, 0:1], in1=gG_rep[:],
-                op0=ALU.subtract, op1=ALU.mult,
+                out=result[:], in0=turned[t][i][:], scalar=mean_var[:, i, 0:1],
+                in1=repeated[:, i, :], op0=ALU.subtract, op1=ALU.mult,
             )
-            y_gain = work.tile([P, WIDTH], F32)
+            return result
+
+        def shift(t, i):
+            source, inv_std = centred[t][i], centred[t][2]
+            result = work.tile([P, WIDTH], F32, name="normed%d" % i)
             nc.vector.scalar_tensor_tensor(
-                out=y_gain[:], in0=y_turned[:], scalar=mean_var[:, 1, 0:1], in1=gE_rep[:],
-                op0=ALU.subtract, op1=ALU.mult,
+                out=result[:], in0=source[:], scalar=inv_std[:, i : i + 1],
+                in1=repeated[:, 2 + i, :], op0=ALU.mult, op1=ALU.add,
             )
-            centred[pair, a] = (x_gain, y_gain, inv_std)
+            normed[t, i] = result
 
-        def norms_second(pair):
-            ge_rows = work.tile([P, 2, WIDTH], BF16)
-            for a in range(2):
-                x_gain, y_gain, inv_std = centred[pair, a]
-                g = work.tile([P, WIDTH], F32)
-                nc.vector.scalar_tensor_tensor(
-                    out=g[:], in0=x_gain[:], scalar=inv_std[:, 0:1], in1=betaG_rep[:],
-                    op0=ALU.mult, op1=ALU.add,
+        def gate(t):
+            pair, a = divmod(t, 2)
+            if a == 0:
+                ge_of[pair] = work.tile([P, 2 * WIDTH], BF16, name="ge_rows")
+            nc.vector.tensor_tensor(
+                out=ge_of[pair][:, a * WIDTH : (a + 1) * WIDTH],
+                in0=normed[t, 0][:], in1=normed[t, 1][:], op=ALU.mult,
+            )
+
+        def norms(t, middle=(), late=()):
+            now, before = t < 2 * PAIRS, t > 0
+            if now:
+                stats = small.tile([P, 2, 6], F32)
+                mean_var = small.tile([P, 2, 2], F32)
+                statistics(t, 0, stats)
+            if before:
+                shift(t - 1, 0)
+            if now:
+                statistics(t, 1, stats)
+                nc.vector.bn_aggr(out=mean_var[:, 0, :], in_=stats[:, 0, :])
+            if before:
+                shift(t - 1, 1)
+            if now:
+                nc.vector.bn_aggr(out=mean_var[:, 1, :], in_=stats[:, 1, :])
+                var_eps = small.tile([P, 2], F32)
+                nc.gpsimd.tensor_scalar(
+                    out=var_eps[:], in0=mean_var[:, :, 1], scalar1=EPS, scalar2=None, op0=ALU.add
                 )
-                e = work.tile([P, WIDTH], F32)
-                nc.vector.scalar_tensor_tensor(
-                    out=e[:], in0=y_gain[:], scalar=inv_std[:, 1:2], in1=betaE_rep[:],
-                    op0=ALU.mult, op1=ALU.add,
+                inv_std = small.tile([P, 2], F32)
+                nc.gpsimd.tensor_tensor(
+                    out=inv_std[:], in0=var_eps[:], in1=minus_half[:], op=ALU.pow
                 )
-                nc.vector.tensor_tensor(out=ge_rows[:, a, :], in0=g[:], in1=e[:], op=ALU.mult)
-            ge_of[pair] = ge_rows
+            for name in middle:
+                quantise(name)
+            if now:
+                x = centre(t, 0, mean_var)
+            if before:
+                gate(t - 1)
+            if now:
+                y = centre(t, 1, mean_var)
+                centred[t] = (x, y, inv_std)
+            for name in late:
+                quantise(name)
 
-        def flip_gate(pair):
-            ge_rows = ge_of[pair]
-            grouped = work.tile([P, PAIR * PACK], BF16, name="ge_grouped", align_bytes=64)
-            flip_two_tiles(
-                ge_rows[:].rearrange("p a (l r) -> p a l r", l=BF16_LANES),
-                BF16_LANES,
-                grouped[:].rearrange("p (a r l) -> p a r l", a=2, l=BF16_LANES),
-                True,
-            )
-            flipped_rows["ge%d" % pair] = grouped
+        def flip_gate(pair, a, tiles):
+            name = "ge_%d" % (pair if tiles == 2 else 2 * pair + a)
+            grouped = work.tile([P, tiles * P * PACK], BF16, name="ge_grouped%d" % tiles, align_bytes=64)
+            rows = ge_of[pair][:, a * WIDTH : (a + tiles) * WIDTH]
+            flip(rows, grouped[:], False, "scalar", banks)
+            grouped_of[name] = grouped
 
-        def store_tile(pair, a):
-            turned = turn_sum(flip_banks, [terms["r3", pair], terms["c", pair]], a)
-            result = work.tile([P, WIDTH], F32, bufs=4)
-            nc.scalar.copy(out=result[:], in_=turned[:])
-            nc.sync.dma_start(out=out_view[:, 2 * pair + a, :], in_=result[:])
+        def gate_term(pair, a, engines):
+            codes, scales = packed["ge_%d" % (2 * pair + a)]
+            if a == 0:
+                terms["c", pair] = major.tile([P, TILES, PAIR], F32, name="c")
+            acc = banks.tile([P, TILES, P], F32, tag="bank")
+            for f in range(TILES):
+                w_codes, w_scales = packed["Wc_%d" % (f // 2)]
+                features = slice((f % 2) * P, (f % 2 + 1) * P)
+                nc.tensor.matmul_mx(
+                    out=acc[:, f, :],
+                    lhsT=w_codes[:, features].bitcast(FP8X4),
+                    lhsT_scale=w_scales[:, features],
+                    rhs=codes[:].bitcast(FP8X4),
+                    rhs_scale=scales[:],
+                    start=True,
+                    stop=True,
+                )
+            for f in range(TILES):
+                add_bias_relu(
+                    engines[f], terms["c", pair][:, f, a * P : (a + 1) * P], acc[:, f, :], 1, TILES + f
+                )
 
-        operand("W0")
-        operand("q0")
-        operand("q_hat0")
+        def store_tile(pair, a, engines=("scalar",)):
+            bank = banks.tile([P, WIDTH], F32, tag="bank")
+            turn_sum(bank, [terms["r3", pair], terms["c", pair]], a)
+            width = WIDTH // len(engines)
+            for i, engine in enumerate(engines):
+                cols = slice(i * width, (i + 1) * width)
+                result = work.tile([P, width], F32, name="result%d" % width, bufs=4)
+                if engine == "scalar":
+                    nc.scalar.copy(out=result[:], in_=bank[:, cols])
+                else:
+                    nc.vector.tensor_copy(out=result[:], in_=bank[:, cols])
+                nc.sync.dma_start(out=out_view[:, 2 * pair + a, cols], in_=result[:])
 
-        bias_flipped = flip_banks.tile([P, P], BF16, tag="bank")
-        nc.tensor.transpose(bias_flipped[:], bias_rows[:], ident_bf16[:])
-        bias_cols = const.tile([P, P], F32)
-        nc.vector.tensor_copy(out=bias_cols[:], in_=bias_flipped[:])
+        repeated = const.tile([P, 4, WIDTH], BF16)
+        spread = {}
 
-        operand("W1")
-        relu_term("r0", "W0", "q", 0, 0)
-        operand("W2")
-        relu_term("r1", "W1", "q_hat", 1, 0)
-        relu_term("y", "W2", "q_hat", 2, 0)
-        turn_tile(0, 0)
+        def repeat_rows(half):
+            spread[half] = norm_banks.tile([P, 2, WIDTH], BF16, tag="bank", name="spread")
+            for i in range(2):
+                j = 2 * half + i
+                nc.tensor.matmul(
+                    out=spread[half][:, i, :],
+                    lhsT=ident_bf16[:, j : j + 1].to_broadcast([P, P]),
+                    rhs=norm_rows[:],
+                    start=True,
+                    stop=True,
+                )
 
-        repeated = []
-        for j in range(4):
-            spread = mx_banks.tile([P, WIDTH], F32, tag="acc")
-            nc.tensor.matmul(
-                out=spread[:],
-                lhsT=ident_bf16[:, j : j + 1].to_broadcast([P, P]),
-                rhs=norm_rows[:],
-                start=True,
-                stop=True,
-            )
-            row = const.tile([P, WIDTH], F32, name="repeated%d" % j)
-            nc.scalar.copy(out=row[:], in_=spread[:])
-            repeated.append(row)
-        gG_rep, gE_rep, betaG_rep, betaE_rep = repeated
+        def copy_repeated(half, engine):
+            target = repeated[:, 2 * half : 2 * half + 2, :]
+            if engine == "scalar":
+                nc.scalar.copy(out=target, in_=spread[half][:])
+            else:
+                nc.vector.tensor_copy(out=target, in_=spread[half][:])
 
+        bias_cols = []
 
-        turn_tile(0, 1)
-        flip_tokens(1)
-        norms_first(0, 0)
-        norms_first(0, 1)
-        relu_term("r0", "W0", "q", 0, 1)
-        relu_term("r1", "W1", "q_hat", 1, 1)
-        relu_term("y", "W2", "q_hat", 2, 1)
-        flip_tokens(2)
-        flip_rows("W3", vector_helps=False)
-        flip_rows("Wc", BF16_LANES, vector_helps=False)
+        def flip_bias(i, engine):
+            bias_flipped = banks.tile([P, P], BF16, tag="bank")
+            nc.tensor.transpose(bias_flipped[:], bias_rows[i][:], ident_bf16[:])
+            cols = const.tile([P, P], F32, name="bias_cols%d" % i)
+            if engine == "scalar":
+                nc.scalar.copy(out=cols[:], in_=bias_flipped[:])
+            else:
+                nc.vector.tensor_copy(out=cols[:], in_=bias_flipped[:])
+            bias_cols.append(cols)
 
-        def exists(pair):
-            return 0 <= pair < PAIRS
+        flip_rows("q_0", "vector")
+        flip_rows("W0_0", "scalar")
+        quantise("q_0")
+        flip_rows("W0_1", "vector")
+        quantise("W0_0")
+        quantise("W0_1")
+        flip_rows("h_0", "scalar")
+        flip_rows("W1_0", "vector", norm_banks)
+        quantise("h_0")
+        flip_rows("W1_1", "scalar", norm_banks)
+        quantise("W1_0")
+        flip_bias(0, "vector")
+        relu_half("r0", 0, 0, "scalar")
+        flip_rows("W2_0", "vector", norm_banks)
+        quantise("W1_1")
+        flip_rows("W2_1", "scalar", norm_banks)
+        quantise("W2_0")
+        relu_half("r0", 0, 1, "scalar")
+        relu_half("r1", 0, 0, "scalar")
+        quantise("W2_1")
+        repeat_rows(0)
+        relu_half("r1", 0, 1, "vector")
+        relu_half("y", 0, 0, "scalar")
+        relu_half("y", 0, 1, "vector")
+        turn_tile(0)
+        copy_repeated(0, "scalar")
+        repeat_rows(1)
+        copy_repeated(1, "scalar")
+        flip_rows("q_1", "scalar")
+        flip_rows("h_1", "scalar")
+        turn_tile(1)
+        norms(0, late=("q_1", "h_1"))
+        flip_bias(1, "scalar")
+        relu_term("r0", 1)
+        relu_term("r1", 1)
+        relu_term("y", 1)
+        flip_rows("W3_0", "scalar")
+        flip_rows("W3_1", "scalar")
+        flip_rows("q_2", "scalar")
+        flip_rows("h_2", "scalar")
+        turn_tile(2)
+        norms(1, late=("W3_0", "W3_1", "q_2", "h_2"))
+        relu_term("r0", 2)
 
-        for s in range(PAIRS + 2):
-            if exists(s):
-                norms_second(s)
-            if exists(s + 1):
-                turn_tile(s + 1, 0)
-            if exists(s - 1):
-                relu_term("r3", "W3", "q", 3, s - 1)
-            if exists(s + 1):
-                turn_tile(s + 1, 1)
-            if exists(s - 1):
-                relu_term("c", "Wc", "ge", 4, s - 1)
-            if exists(s + 2):
-                relu_term("r0", "W0", "q", 0, s + 2)
-            if exists(s - 2):
+        for s in range(1, PAIRS):
+            last = s == PAIRS - 1
+            turn_tile(2 * s + 1)
+            if s > 1:
                 store_tile(s - 2, 0)
-            if exists(s + 2):
-                relu_term("r1", "W1", "q_hat", 1, s + 2)
-            if exists(s - 2):
+            if last:
+                relu_term("r3", s - 1)
+            else:
+                relu_term("r1", s + 1)
+            if s > 1:
                 store_tile(s - 2, 1)
-            if exists(s + 2):
-                relu_term("y", "W2", "q_hat", 2, s + 2)
-            if exists(s + 3):
-                flip_tokens(s + 3)
-            if exists(s):
-                flip_gate(s)
-            if exists(s + 1):
-                norms_first(s + 1, 0)
-                norms_first(s + 1, 1)
+            if last:
+                relu_term("r3", s)
+            else:
+                relu_term("y", s + 1)
+            if s == 1:
+                flip_rows("Wc_0", "scalar")
+                flip_rows("Wc_1", "scalar")
+                flip_rows("q_3", "scalar")
+                flip_rows("h_3", "scalar")
+            norms(2 * s, late=("Wc_0", "Wc_1", "q_3", "h_3") if s == 1 else ())
+            flip_gate(s - 1, 0, 2)
+            if not last:
+                turn_tile(2 * s + 2)
+                relu_term("r3", s - 1)
+            norms(2 * s + 1, middle=("ge_%d" % (s - 1),))
+            if s + 2 < PAIRS:
+                relu_term("r0", s + 2)
+            relu_term("c", s - 1)
+
+        s = PAIRS - 1
+        flip_gate(s, 0, 1)
+        shift(2 * s + 1, 0)
+        quantise("ge_%d" % (2 * s))
+        store_tile(s - 1, 0)
+        gate_term(s, 0, ("scalar", "scalar", "scalar", "scalar"))
+        shift(2 * s + 1, 1)
+        gate(2 * s + 1)
+        store_tile(s - 1, 1)
+        flip_gate(s, 1, 1)
+        quantise("ge_%d" % (2 * s + 1))
+        store_tile(s, 0)
+        gate_term(s, 1, ("scalar", "vector", "scalar", "vector"))
+        store_tile(s, 1, ("scalar", "vector"))

@@ -51,8 +51,8 @@ def tile_pregatingcontextualattentiongate_pb_kernel(
             nc.vector.memset(rows[:], 0.0)
         norm_rows = const.tile([P, WIDTH], BF16)
         nc.vector.memset(norm_rows[:], 0.0)
-        minus_half = const.tile([P, 2], F32)
-        nc.vector.memset(minus_half[:], -0.5)
+        ones = const.tile([P, 2], F32)
+        nc.vector.memset(ones[:], 1.0)
         ident_f32 = const.tile([P, P], F32)
         make_identity(nc, ident_f32[:])
         ident_bf16 = const.tile([P, P], BF16)
@@ -89,6 +89,10 @@ def tile_pregatingcontextualattentiongate_pb_kernel(
         load_bias(nc.scalar, 0, 0, b0)
         load_bias(nc.scalar, 0, 1, b1)
         load_weight("W2")
+        for j, v in enumerate([gG, gE, betaG, betaE]):
+            nc.sync.dma_start(
+                out=norm_rows[j : j + 1, :], in_=v.rearrange("(o c) -> o c", o=1)
+            )
         load_tokens("q", 1)
         load_tokens("h", 1)
         load_weight("W3")
@@ -99,15 +103,11 @@ def tile_pregatingcontextualattentiongate_pb_kernel(
         load_tokens("h", 3)
 
         load_bias(nc.gpsimd, 0, 2, b2)
-        for j, v in enumerate([gG, gE, betaG, betaE]):
-            nc.gpsimd.dma_start(
-                out=norm_rows[j : j + 1, :], in_=v.rearrange("(o c) -> o c", o=1)
-            )
         load_bias(nc.gpsimd, 1, 0, b3)
         load_bias(nc.gpsimd, 1, 1, bc)
         table_loader = const.tile([P, 2], F32)
         nc.scalar.activation(
-            out=table_loader[:], in_=minus_half[:], func=ACT.Relu, bias=0.0, scale=1.0
+            out=table_loader[:], in_=ones[:], func=ACT.Abs_reciprocal_sqrt, bias=0.0, scale=1.0
         )
 
         packed = {}
@@ -257,13 +257,10 @@ def tile_pregatingcontextualattentiongate_pb_kernel(
                 shift(t - 1, 1)
             if now:
                 nc.vector.bn_aggr(out=mean_var[:, 1, :], in_=stats[:, 1, :])
-                var_eps = small.tile([P, 2], F32)
-                nc.gpsimd.tensor_scalar(
-                    out=var_eps[:], in0=mean_var[:, :, 1], scalar1=EPS, scalar2=None, op0=ALU.add
-                )
                 inv_std = small.tile([P, 2], F32)
-                nc.gpsimd.tensor_tensor(
-                    out=inv_std[:], in0=var_eps[:], in1=minus_half[:], op=ALU.pow
+                nc.scalar.activation(
+                    out=inv_std[:], in_=mean_var[:, :, 1], func=ACT.Abs_reciprocal_sqrt,
+                    bias=EPS, scale=1.0,
                 )
             for name in middle:
                 quantise(name)
@@ -373,11 +370,11 @@ def tile_pregatingcontextualattentiongate_pb_kernel(
         relu_half("r0", 0, 1, "scalar")
         relu_half("r1", 0, 0, "scalar")
         quantise("W2_1")
-        repeat_rows(0)
         relu_half("r1", 0, 1, "vector")
         relu_half("y", 0, 0, "scalar")
         relu_half("y", 0, 1, "vector")
         turn_tile(0)
+        repeat_rows(0)
         copy_repeated(0, "scalar")
         repeat_rows(1)
         copy_repeated(1, "scalar")
@@ -387,45 +384,55 @@ def tile_pregatingcontextualattentiongate_pb_kernel(
         norms(0, late=("q_1", "h_1"))
         flip_bias(1, "scalar")
         relu_term("r0", 1)
+        norms(1)
         relu_term("r1", 1)
         relu_term("y", 1)
-        flip_rows("W3_0", "scalar")
-        flip_rows("W3_1", "scalar")
+
         flip_rows("q_2", "scalar")
         flip_rows("h_2", "scalar")
         turn_tile(2)
-        norms(1, late=("W3_0", "W3_1", "q_2", "h_2"))
+        norms(2, middle=("q_2", "h_2"))
         relu_term("r0", 2)
+        turn_tile(3)
+        relu_term("r1", 2)
 
-        for s in range(1, PAIRS):
-            last = s == PAIRS - 1
-            turn_tile(2 * s + 1)
-            if s > 1:
-                store_tile(s - 2, 0)
-            if last:
-                relu_term("r3", s - 1)
-            else:
-                relu_term("r1", s + 1)
-            if s > 1:
-                store_tile(s - 2, 1)
-            if last:
-                relu_term("r3", s)
-            else:
-                relu_term("y", s + 1)
-            if s == 1:
-                flip_rows("Wc_0", "scalar")
-                flip_rows("Wc_1", "scalar")
-                flip_rows("q_3", "scalar")
-                flip_rows("h_3", "scalar")
-            norms(2 * s, late=("Wc_0", "Wc_1", "q_3", "h_3") if s == 1 else ())
-            flip_gate(s - 1, 0, 2)
-            if not last:
-                turn_tile(2 * s + 2)
-                relu_term("r3", s - 1)
-            norms(2 * s + 1, middle=("ge_%d" % (s - 1),))
-            if s + 2 < PAIRS:
-                relu_term("r0", s + 2)
-            relu_term("c", s - 1)
+        flip_rows("W3_0", "scalar")
+        flip_rows("W3_1", "scalar")
+        flip_gate(0, 0, 2)
+        relu_term("y", 2)
+        norms(3, middle=("ge_0", "W3_0", "W3_1"))
+        flip_rows("q_3", "scalar")
+        flip_rows("h_3", "scalar")
+        turn_tile(4)
+
+        flip_rows("Wc_0", "scalar")
+        flip_rows("Wc_1", "scalar")
+        norms(4, middle=("q_3", "h_3"), late=("Wc_0", "Wc_1"))
+        relu_term("r0", 3)
+        turn_tile(5)
+        relu_term("r1", 3)
+        relu_term("r3", 0)
+
+        flip_gate(1, 0, 2)
+        relu_term("y", 3)
+        relu_term("c", 0)
+        norms(5, middle=("ge_1",))
+        turn_tile(6)
+        relu_term("r3", 1)
+
+        store_tile(0, 0)
+        relu_term("c", 1)
+        store_tile(0, 1)
+        norms(6)
+        turn_tile(7)
+        relu_term("r3", 2)
+
+        flip_gate(2, 0, 2)
+        store_tile(1, 0)
+        relu_term("r3", 3)
+        norms(7, middle=("ge_2",))
+        store_tile(1, 1)
+        relu_term("c", 2)
 
         s = PAIRS - 1
         flip_gate(s, 0, 1)

@@ -166,7 +166,7 @@ def tile_pregatingcontextualattentiongate_pb_kernel(
             w_codes, w_scales = packed["%s_%d" % (weight, half)]
             t_codes, t_scales = packed["%s_%d" % (tokens, pair)]
             if half == 0:
-                terms[name, pair] = major.tile([P, TILES, PAIR], F32, name=name)
+                terms[name, pair] = major.tile([P, TILES, PAIR], F32, name=name, bufs=4)
             result = terms[name, pair]
             acc = banks.tile([P, 2, PAIR], F32, tag="bank")
             for i in range(2):
@@ -201,6 +201,8 @@ def tile_pregatingcontextualattentiongate_pb_kernel(
                     )
 
         turned = {}
+        moments = {}
+        inverse = {}
         centred = {}
         normed = {}
         ge_of = {}
@@ -225,7 +227,7 @@ def tile_pregatingcontextualattentiongate_pb_kernel(
             return result
 
         def shift(t, i):
-            source, inv_std = centred[t][i], centred[t][2]
+            source, inv_std = centred[t][i], inverse[t]
             result = work.tile([P, WIDTH], F32, name="normed%d" % i)
             nc.vector.scalar_tensor_tensor(
                 out=result[:], in0=source[:], scalar=inv_std[:, i : i + 1],
@@ -247,6 +249,7 @@ def tile_pregatingcontextualattentiongate_pb_kernel(
             if now:
                 stats = small.tile([P, 2, 6], F32)
                 mean_var = small.tile([P, 2, 2], F32)
+                moments[t] = mean_var
                 statistics(t, 0, stats)
             if before:
                 shift(t - 1, 0)
@@ -257,11 +260,6 @@ def tile_pregatingcontextualattentiongate_pb_kernel(
                 shift(t - 1, 1)
             if now:
                 nc.vector.bn_aggr(out=mean_var[:, 1, :], in_=stats[:, 1, :])
-                inv_std = small.tile([P, 2], F32)
-                nc.scalar.activation(
-                    out=inv_std[:], in_=mean_var[:, :, 1], func=ACT.Abs_reciprocal_sqrt,
-                    bias=EPS, scale=1.0,
-                )
             for name in middle:
                 quantise(name)
             if now:
@@ -270,9 +268,17 @@ def tile_pregatingcontextualattentiongate_pb_kernel(
                 gate(t - 1)
             if now:
                 y = centre(t, 1, mean_var)
-                centred[t] = (x, y, inv_std)
+                centred[t] = (x, y)
             for name in late:
                 quantise(name)
+
+        def invert(t):
+            inv_std = small.tile([P, 2], F32)
+            nc.scalar.activation(
+                out=inv_std[:], in_=moments[t][:, :, 1], func=ACT.Abs_reciprocal_sqrt,
+                bias=EPS, scale=1.0,
+            )
+            inverse[t] = inv_std
 
         def flip_gate(pair, a, tiles):
             name = "ge_%d" % (pair if tiles == 2 else 2 * pair + a)
@@ -284,7 +290,7 @@ def tile_pregatingcontextualattentiongate_pb_kernel(
         def gate_term(pair, a, engines):
             codes, scales = packed["ge_%d" % (2 * pair + a)]
             if a == 0:
-                terms["c", pair] = major.tile([P, TILES, PAIR], F32, name="c")
+                terms["c", pair] = major.tile([P, TILES, PAIR], F32, name="c", bufs=4)
             acc = banks.tile([P, TILES, P], F32, tag="bank")
             for f in range(TILES):
                 w_codes, w_scales = packed["Wc_%d" % (f // 2)]
@@ -320,7 +326,7 @@ def tile_pregatingcontextualattentiongate_pb_kernel(
         spread = {}
 
         def repeat_rows(half):
-            spread[half] = norm_banks.tile([P, 2, WIDTH], BF16, tag="bank", name="spread")
+            spread[half] = banks.tile([P, 2, WIDTH], BF16, tag="bank", name="spread")
             for i in range(2):
                 j = 2 * half + i
                 nc.tensor.matmul(
@@ -368,6 +374,7 @@ def tile_pregatingcontextualattentiongate_pb_kernel(
         flip_rows("W2_1", "scalar", norm_banks)
         quantise("W2_0")
         relu_half("r0", 0, 1, "scalar")
+        flip_rows("q_1", "scalar")
         relu_half("r1", 0, 0, "scalar")
         quantise("W2_1")
         relu_half("r1", 0, 1, "vector")
@@ -378,60 +385,69 @@ def tile_pregatingcontextualattentiongate_pb_kernel(
         copy_repeated(0, "scalar")
         repeat_rows(1)
         copy_repeated(1, "scalar")
-        flip_rows("q_1", "scalar")
         flip_rows("h_1", "scalar")
         turn_tile(1)
-        norms(0, late=("q_1", "h_1"))
-        flip_bias(1, "scalar")
+
+        norms(0, middle=("q_1",), late=("h_1",))
         relu_term("r0", 1)
-        norms(1)
+        invert(0)
         relu_term("r1", 1)
-        relu_term("y", 1)
 
         flip_rows("q_2", "scalar")
         flip_rows("h_2", "scalar")
+        norms(1, late=("q_2", "h_2"))
+        relu_term("y", 1)
+        invert(1)
+        flip_bias(1, "scalar")
         turn_tile(2)
-        norms(2, middle=("q_2", "h_2"))
         relu_term("r0", 2)
-        turn_tile(3)
-        relu_term("r1", 2)
 
         flip_rows("W3_0", "scalar")
         flip_rows("W3_1", "scalar")
-        flip_gate(0, 0, 2)
+        norms(2, late=("W3_0", "W3_1"))
+        relu_term("r1", 2)
+        invert(2)
+        turn_tile(3)
         relu_term("y", 2)
-        norms(3, middle=("ge_0", "W3_0", "W3_1"))
+
+        flip_gate(0, 0, 2)
         flip_rows("q_3", "scalar")
         flip_rows("h_3", "scalar")
+        norms(3, middle=("ge_0",), late=("q_3", "h_3"))
+        relu_term("r3", 0)
+        invert(3)
         turn_tile(4)
-
         flip_rows("Wc_0", "scalar")
         flip_rows("Wc_1", "scalar")
-        norms(4, middle=("q_3", "h_3"), late=("Wc_0", "Wc_1"))
+
+        norms(4, late=("Wc_0", "Wc_1"))
         relu_term("r0", 3)
         turn_tile(5)
         relu_term("r1", 3)
-        relu_term("r3", 0)
-
-        flip_gate(1, 0, 2)
-        relu_term("y", 3)
-        relu_term("c", 0)
-        norms(5, middle=("ge_1",))
-        turn_tile(6)
+        invert(4)
         relu_term("r3", 1)
 
+        flip_gate(1, 0, 2)
+        norms(5, middle=("ge_1",))
+        relu_term("y", 3)
+        relu_term("c", 0)
+        invert(5)
+        turn_tile(6)
+
         store_tile(0, 0)
+        norms(6)
         relu_term("c", 1)
         store_tile(0, 1)
-        norms(6)
-        turn_tile(7)
         relu_term("r3", 2)
+        invert(6)
+        turn_tile(7)
+        relu_term("r3", 3)
 
         flip_gate(2, 0, 2)
         store_tile(1, 0)
-        relu_term("r3", 3)
         norms(7, middle=("ge_2",))
         store_tile(1, 1)
+        invert(7)
         relu_term("c", 2)
 
         s = PAIRS - 1

@@ -239,7 +239,8 @@ def tile_pregatingcontextualattentiongate_pb_kernel(
             pair, a = divmod(t, 2)
             if a == 0:
                 ge_of[pair] = work.tile([P, 2 * WIDTH], BF16, name="ge_rows")
-            nc.vector.tensor_tensor(
+            engine = nc.vector if t >= 2 * PAIRS - 2 else nc.gpsimd
+            engine.tensor_tensor(
                 out=ge_of[pair][:, a * WIDTH : (a + 1) * WIDTH],
                 in0=normed[t, 0][:], in1=normed[t, 1][:], op=ALU.mult,
             )

@@ -281,11 +281,11 @@ def tile_pregatingcontextualattentiongate_pb_kernel(
             )
             inverse[t] = inv_std
 
-        def flip_gate(pair, a, tiles):
+        def flip_gate(pair, a, tiles, engine="scalar"):
             name = "ge_%d" % (pair if tiles == 2 else 2 * pair + a)
             grouped = work.tile([P, tiles * P * PACK], BF16, name="ge_grouped%d" % tiles, align_bytes=64)
             rows = ge_of[pair][:, a * WIDTH : (a + tiles) * WIDTH]
-            flip(rows, grouped[:], False, "scalar", banks)
+            flip(rows, grouped[:], False, engine, banks)
             grouped_of[name] = grouped
 
         def gate_term(pair, a, engines):
@@ -312,7 +312,16 @@ def tile_pregatingcontextualattentiongate_pb_kernel(
 
         def store_tile(pair, a, engines=("scalar",)):
             bank = banks.tile([P, WIDTH], F32, tag="bank")
-            turn_sum(bank, [terms["r3", pair], terms["c", pair]], a)
+            parts = [terms["r3", pair], terms["c", pair]]
+            if pair == PAIRS - 2 and a == 1:
+                total = work.tile([P, TILES, P], F32, name="total")
+                cols = slice(a * P, (a + 1) * P)
+                nc.gpsimd.tensor_tensor(
+                    out=total[:], in0=parts[0][:, :, cols], in1=parts[1][:, :, cols], op=ALU.add
+                )
+                turn_sum(bank, [total], 0)
+            else:
+                turn_sum(bank, parts, a)
             width = WIDTH // len(engines)
             for i, engine in enumerate(engines):
                 cols = slice(i * width, (i + 1) * width)
@@ -326,8 +335,8 @@ def tile_pregatingcontextualattentiongate_pb_kernel(
         repeated = const.tile([P, 4, WIDTH], BF16)
         spread = {}
 
-        def repeat_rows(half):
-            spread[half] = banks.tile([P, 2, WIDTH], BF16, tag="bank", name="spread")
+        def repeat_rows(half, pool):
+            spread[half] = pool.tile([P, 2, WIDTH], BF16, tag="bank", name="spread")
             for i in range(2):
                 j = 2 * half + i
                 nc.tensor.matmul(
@@ -375,23 +384,23 @@ def tile_pregatingcontextualattentiongate_pb_kernel(
         flip_rows("W2_1", "scalar", norm_banks)
         quantise("W2_0")
         relu_half("r0", 0, 1, "scalar")
-        flip_rows("q_1", "scalar")
         relu_half("r1", 0, 0, "scalar")
         quantise("W2_1")
         relu_half("r1", 0, 1, "vector")
         relu_half("y", 0, 0, "scalar")
         relu_half("y", 0, 1, "vector")
+        repeat_rows(0, norm_banks)
         turn_tile(0)
-        repeat_rows(0)
         copy_repeated(0, "scalar")
-        repeat_rows(1)
-        copy_repeated(1, "scalar")
+        flip_rows("q_1", "scalar")
         flip_rows("h_1", "scalar")
+        repeat_rows(1, banks)
+        copy_repeated(1, "scalar")
         turn_tile(1)
 
-        norms(0, middle=("q_1",), late=("h_1",))
-        relu_term("r0", 1)
+        norms(0, middle=("q_1", "h_1"))
         invert(0)
+        relu_term("r0", 1)
         relu_term("r1", 1)
 
         flip_rows("q_2", "scalar")
@@ -434,14 +443,14 @@ def tile_pregatingcontextualattentiongate_pb_kernel(
         relu_term("c", 0)
         invert(5)
         turn_tile(6)
+        relu_term("r3", 2)
 
         store_tile(0, 0)
         norms(6)
-        relu_term("c", 1)
-        store_tile(0, 1)
-        relu_term("r3", 2)
-        invert(6)
         turn_tile(7)
+        relu_term("c", 1)
+        invert(6)
+        store_tile(0, 1)
         relu_term("r3", 3)
 
         flip_gate(2, 0, 2)
@@ -454,14 +463,14 @@ def tile_pregatingcontextualattentiongate_pb_kernel(
         s = PAIRS - 1
         flip_gate(s, 0, 1)
         shift(2 * s + 1, 0)
-        quantise("ge_%d" % (2 * s))
-        store_tile(s - 1, 0)
-        gate_term(s, 0, ("scalar", "scalar", "scalar", "scalar"))
         shift(2 * s + 1, 1)
         gate(2 * s + 1)
-        store_tile(s - 1, 1)
-        flip_gate(s, 1, 1)
+        store_tile(s - 1, 0)
+        quantise("ge_%d" % (2 * s))
+        flip_gate(s, 1, 1, "vector")
         quantise("ge_%d" % (2 * s + 1))
-        store_tile(s, 0)
+        gate_term(s, 0, ("scalar", "scalar", "scalar", "scalar"))
+        store_tile(s - 1, 1)
         gate_term(s, 1, ("scalar", "vector", "scalar", "vector"))
+        store_tile(s, 0)
         store_tile(s, 1, ("scalar", "vector"))

@@ -158,11 +158,45 @@ def tile_pregatingcontextualattentiongate_pb_kernel(
                     out=target, in0=source, scalar1=bias, scalar2=0.0, op0=ALU.add, op1=ALU.max
                 )
 
+        sources = {
+            "r0": ("W0", "q", (0, 0)), "r1": ("W1", "h", (0, 1)), "y": ("W2", "h", (0, 2)),
+            "r3": ("W3", "q", (1, 0)), "c": ("Wc", "ge", (1, 1)),
+        }
+
+        def relu_tile(name, t, engines=("scalar",)):
+            weight, tokens, (i_bias, j) = sources[name]
+            pair, a = divmod(t, 2)
+            if name == "c":
+                t_codes, t_scales = packed["ge_%d" % t]
+                columns = slice(0, P)
+            else:
+                t_codes, t_scales = packed["%s_%d" % (tokens, pair)]
+                columns = slice(a * P, (a + 1) * P)
+            if a == 0:
+                terms[name, pair] = major.tile([P, TILES, PAIR], F32, name=name, bufs=4)
+            share = TILES // len(engines)
+            for i, engine in enumerate(engines):
+                acc = banks.tile([P, share, P], F32, tag="bank")
+                for k in range(share):
+                    f = i * share + k
+                    w_codes, w_scales = packed["%s_%d" % (weight, f // 2)]
+                    features = slice((f % 2) * P, (f % 2 + 1) * P)
+                    nc.tensor.matmul_mx(
+                        out=acc[:, k, :],
+                        lhsT=w_codes[:, features].bitcast(FP8X4),
+                        lhsT_scale=w_scales[:, features],
+                        rhs=t_codes[:, columns].bitcast(FP8X4),
+                        rhs_scale=t_scales[:, columns],
+                        start=True,
+                        stop=True,
+                    )
+                for k in range(share):
+                    f = i * share + k
+                    target = terms[name, pair][:, f, a * P : (a + 1) * P]
+                    add_bias_relu(engine, target, acc[:, k, :], i_bias, j * TILES + f)
+
         def relu_half(name, pair, half, engine):
-            weight, tokens, (i_bias, j) = {
-                "r0": ("W0", "q", (0, 0)), "r1": ("W1", "h", (0, 1)), "y": ("W2", "h", (0, 2)),
-                "r3": ("W3", "q", (1, 0)), "c": ("Wc", "ge", (1, 1)),
-            }[name]
+            weight, tokens, (i_bias, j) = sources[name]
             w_codes, w_scales = packed["%s_%d" % (weight, half)]
             t_codes, t_scales = packed["%s_%d" % (tokens, pair)]
             if half == 0:
@@ -188,11 +222,11 @@ def tile_pregatingcontextualattentiongate_pb_kernel(
             for half in range(2):
                 relu_half(name, pair, half, "scalar")
 
-        def turn_sum(bank, parts, a):
-            for f in range(TILES):
+        def turn_sum(bank, parts, a, features=range(TILES)):
+            for k, f in enumerate(features):
                 for i, part in enumerate(parts):
                     nc.tensor.matmul(
-                        out=bank[:, f * P : (f + 1) * P],
+                        out=bank[:, k * P : (k + 1) * P],
                         lhsT=part[:, f, a * P : (a + 1) * P],
                         rhs=ident_f32[:],
                         is_transpose=True,
@@ -288,48 +322,26 @@ def tile_pregatingcontextualattentiongate_pb_kernel(
             flip(rows, grouped[:], False, engine, banks)
             grouped_of[name] = grouped
 
-        def gate_term(pair, a, engines):
-            codes, scales = packed["ge_%d" % (2 * pair + a)]
-            if a == 0:
-                terms["c", pair] = major.tile([P, TILES, PAIR], F32, name="c", bufs=4)
-            acc = banks.tile([P, TILES, P], F32, tag="bank")
-            for f in range(TILES):
-                w_codes, w_scales = packed["Wc_%d" % (f // 2)]
-                features = slice((f % 2) * P, (f % 2 + 1) * P)
-                nc.tensor.matmul_mx(
-                    out=acc[:, f, :],
-                    lhsT=w_codes[:, features].bitcast(FP8X4),
-                    lhsT_scale=w_scales[:, features],
-                    rhs=codes[:].bitcast(FP8X4),
-                    rhs_scale=scales[:],
-                    start=True,
-                    stop=True,
-                )
-            for f in range(TILES):
-                add_bias_relu(
-                    engines[f], terms["c", pair][:, f, a * P : (a + 1) * P], acc[:, f, :], 1, TILES + f
-                )
-
-        def store_tile(pair, a, engines=("scalar",)):
-            bank = banks.tile([P, WIDTH], F32, tag="bank")
-            parts = [terms["r3", pair], terms["c", pair]]
-            if pair == PAIRS - 2 and a == 1:
+        def store_tile(pair, a, engines=("scalar",), on_gpsimd=False):
+            parts, tile = [terms["r3", pair], terms["c", pair]], a
+            if on_gpsimd:
                 total = work.tile([P, TILES, P], F32, name="total")
                 cols = slice(a * P, (a + 1) * P)
                 nc.gpsimd.tensor_tensor(
                     out=total[:], in0=parts[0][:, :, cols], in1=parts[1][:, :, cols], op=ALU.add
                 )
-                turn_sum(bank, [total], 0)
-            else:
-                turn_sum(bank, parts, a)
-            width = WIDTH // len(engines)
+                parts, tile = [total], 0
+            share = TILES // len(engines)
+            width = share * P
             for i, engine in enumerate(engines):
-                cols = slice(i * width, (i + 1) * width)
+                bank = banks.tile([P, width], F32, tag="bank")
+                turn_sum(bank, parts, tile, range(i * share, (i + 1) * share))
                 result = work.tile([P, width], F32, name="result%d" % width, bufs=4)
                 if engine == "scalar":
-                    nc.scalar.copy(out=result[:], in_=bank[:, cols])
+                    nc.scalar.copy(out=result[:], in_=bank[:])
                 else:
-                    nc.vector.tensor_copy(out=result[:], in_=bank[:, cols])
+                    nc.vector.tensor_copy(out=result[:], in_=bank[:])
+                cols = slice(i * width, (i + 1) * width)
                 nc.sync.dma_start(out=out_view[:, 2 * pair + a, cols], in_=result[:])
 
         repeated = const.tile([P, 4, WIDTH], BF16)
@@ -423,7 +435,7 @@ def tile_pregatingcontextualattentiongate_pb_kernel(
         flip_gate(0, 0, 2)
         flip_rows("q_3", "scalar")
         flip_rows("h_3", "scalar")
-        norms(3, middle=("ge_0",), late=("q_3", "h_3"))
+        norms(3, late=("q_3", "h_3", "ge_0"))
         relu_term("r3", 0)
         invert(3)
         turn_tile(4)
@@ -438,7 +450,7 @@ def tile_pregatingcontextualattentiongate_pb_kernel(
         relu_term("r3", 1)
 
         flip_gate(1, 0, 2)
-        norms(5, middle=("ge_1",))
+        norms(5, late=("ge_1",))
         relu_term("y", 3)
         relu_term("c", 0)
         invert(5)
@@ -469,8 +481,8 @@ def tile_pregatingcontextualattentiongate_pb_kernel(
         quantise("ge_%d" % (2 * s))
         flip_gate(s, 1, 1, "vector")
         quantise("ge_%d" % (2 * s + 1))
-        gate_term(s, 0, ("scalar", "scalar", "scalar", "scalar"))
+        relu_tile("c", 2 * s)
         store_tile(s - 1, 1)
-        gate_term(s, 1, ("scalar", "vector", "scalar", "vector"))
+        relu_tile("c", 2 * s + 1, ("scalar", "vector"))
         store_tile(s, 0)
         store_tile(s, 1, ("scalar", "vector"))

@@ -51,6 +51,8 @@ def tile_pregatingcontextualattentiongate_pb_kernel(
             nc.vector.memset(rows[:], 0.0)
         norm_rows = const.tile([P, WIDTH], BF16)
         nc.vector.memset(norm_rows[:], 0.0)
+        zeros = const.tile([P, P], F32)
+        nc.vector.memset(zeros[:], 0.0)
         ones = const.tile([P, 2], F32)
         nc.vector.memset(ones[:], 1.0)
         ident_f32 = const.tile([P, P], F32)
@@ -110,11 +112,16 @@ def tile_pregatingcontextualattentiongate_pb_kernel(
             out=table_loader[:], in_=ones[:], func=ACT.Abs_reciprocal_sqrt, bias=0.0, scale=1.0
         )
 
+        def warm(bank, times):
+            for i in range(times):
+                nc.tensor.matmul(out=bank, lhsT=zeros[:], rhs=zeros[:], start=True, stop=True)
+
         packed = {}
 
-        def flip(rows, grouped, is_weight, engine, pool):
+        def flip(rows, grouped, is_weight, engine, pool, dummies=0):
             tiles = rows.shape[1] // WIDTH
             flipped = pool.tile([P, tiles, 2, P], F32, tag="bank")
+            warm(flipped[:, 0, 0, :], dummies)
             words = rows.bitcast(F32).rearrange("p (a l r) -> p a l r", a=tiles, l=2)
             for a in range(tiles):
                 for l in range(2):
@@ -133,9 +140,9 @@ def tile_pregatingcontextualattentiongate_pb_kernel(
 
         grouped_of = {}
 
-        def flip_rows(name, engine, pool=banks):
+        def flip_rows(name, engine, pool=banks, dummies=0):
             grouped = grouped_pool.tile([P, PAIR * PACK], BF16, name="grouped_" + name, align_bytes=64)
-            flip(raw_of[name], grouped[:], name[0] == "W", engine, pool)
+            flip(raw_of[name], grouped[:], name[0] == "W", engine, pool, dummies)
             grouped_of[name] = grouped
 
         def quantise(name):
@@ -319,7 +326,7 @@ def tile_pregatingcontextualattentiongate_pb_kernel(
             name = "ge_%d" % (pair if tiles == 2 else 2 * pair + a)
             grouped = work.tile([P, tiles * P * PACK], BF16, name="ge_grouped%d" % tiles, align_bytes=64)
             rows = ge_of[pair][:, a * WIDTH : (a + tiles) * WIDTH]
-            flip(rows, grouped[:], False, engine, banks)
+            flip(rows, grouped[:], False, engine, banks, 2 if pair == PAIRS - 1 and a == 1 else 0)
             grouped_of[name] = grouped
 
         def store_tile(pair, a, engines=("scalar",), on_gpsimd=False):
@@ -378,14 +385,14 @@ def tile_pregatingcontextualattentiongate_pb_kernel(
                 nc.vector.tensor_copy(out=cols[:], in_=bias_flipped[:])
             bias_cols.append(cols)
 
-        flip_rows("q_0", "vector")
+        flip_rows("q_0", "vector", dummies=5)
         flip_rows("W0_0", "scalar")
         quantise("q_0")
         flip_rows("W0_1", "vector")
         quantise("W0_0")
         quantise("W0_1")
         flip_rows("h_0", "scalar")
-        flip_rows("W1_0", "vector", norm_banks)
+        flip_rows("W1_0", "vector", norm_banks, dummies=2)
         quantise("h_0")
         flip_rows("W1_1", "scalar", norm_banks)
         quantise("W1_0")

import concourse.mybir as mybir
from concourse.masks import make_identity

F32 = mybir.dt.float32
BF16 = mybir.dt.bfloat16
U32 = mybir.dt.uint32
U8 = mybir.dt.uint8
FP8X4 = mybir.dt.float8_e4m3fn_x4
ALU = mybir.AluOpType
ACT = mybir.ActivationFunctionType

P = 128
PACK = 4
TOKENS = 1024
WIDTH = 512
TILES = WIDTH // P
PAIR = 2 * P
PAIRS = TOKENS // PAIR
EPS = 1e-5

FLOPS = 5 * 2 * TOKENS * WIDTH * WIDTH


def tile_pregatingcontextualattentiongate_pb_kernel(
    tc, q, q_hat, W0, b0, W1, b1, W2, b2, W3, b3, gG, betaG, gE, betaE, Wc, bc, out
):
    nc = tc.nc

    token_tiles = TOKENS // P
    views = {
        "q": q.flatten_outer_dims().rearrange("(p r) k -> p r k", r=token_tiles),
        "h": q_hat.flatten_outer_dims().rearrange("(p r) k -> p r k", r=token_tiles),
    }
    out_view = out.flatten_outer_dims().rearrange("(p r) f -> p r f", r=token_tiles)
    weights = {"W0": W0, "W1": W1, "W2": W2, "W3": W3, "Wc": Wc}

    with (
        tc.tile_pool(name="const", bufs=1) as const,
        tc.tile_pool(name="raw", bufs=1) as raw_pool,
        tc.tile_pool(name="grouped", bufs=1) as grouped_pool,
        tc.tile_pool(name="operands", bufs=1) as operands,
        tc.tile_pool(name="major", bufs=2) as major,
        tc.tile_pool(name="work", bufs=2) as work,
        tc.tile_pool(name="small", bufs=4) as small,
        tc.psum_pool(name="banks", bufs=4) as banks,
        tc.psum_pool(name="norm_banks", bufs=4) as norm_banks,
        tc.manual_schedule(),
    ):
        bias_rows = [const.tile([P, P], BF16, name="bias_rows%d" % i) for i in range(2)]
        for rows in bias_rows:
            nc.vector.memset(rows[:], 0.0)
        norm_rows = const.tile([P, WIDTH], BF16)
        nc.vector.memset(norm_rows[:], 0.0)
        zeros = const.tile([P, P], F32)
        nc.vector.memset(zeros[:], 0.0)
        ones = const.tile([P, 2], F32)
        nc.vector.memset(ones[:], 1.0)
        ident_f32 = const.tile([P, P], F32)
        make_identity(nc, ident_f32[:])
        ident_bf16 = const.tile([P, P], BF16)
        nc.vector.tensor_copy(out=ident_bf16[:], in_=ident_f32[:])

        raw_of = {}

        def load(name, view):
            raw = raw_pool.tile([P, 2 * WIDTH], BF16, name="raw_" + name)
            nc.sync.dma_start(out=raw[:].rearrange("p (a k) -> p a k", a=2), in_=view)
            raw_of[name] = raw[:]

        def load_half(name, half):
            rows = weights[name][half * PAIR : (half + 1) * PAIR, :]
            load("%s_%d" % (name, half), rows.rearrange("(p a) k -> p a k", a=2))

        def load_weight(name):
            for half in range(2):
                load_half(name, half)

        def load_tokens(name, pair):
            load("%s_%d" % (name, pair), views[name][:, 2 * pair : 2 * pair + 2, :])

        def load_bias(queue, i, j, b):
            queue.dma_start(
                out=bias_rows[i][j * TILES : (j + 1) * TILES, :],
                in_=b.rearrange("(f c) -> f c", c=P),
            )

        load_tokens("q", 0)
        load_weight("W0")
        load_tokens("h", 0)
        load_weight("W1")
        load_bias(nc.scalar, 0, 0, b0)
        load_bias(nc.scalar, 0, 1, b1)
        load_weight("W2")
        for j, v in enumerate([gG, gE, betaG, betaE]):
            nc.sync.dma_start(
                out=norm_rows[j : j + 1, :], in_=v.rearrange("(o c) -> o c", o=1)
            )
        load_tokens("q", 1)
        load_tokens("h", 1)
        load_weight("W3")
        load_tokens("q", 2)
        load_tokens("h", 2)
        load_weight("Wc")
        load_tokens("q", 3)
        load_tokens("h", 3)

        load_bias(nc.gpsimd, 0, 2, b2)
        load_bias(nc.gpsimd, 1, 0, b3)
        load_bias(nc.gpsimd, 1, 1, bc)
        table_loader = const.tile([P, 2], F32)
        nc.scalar.activation(
            out=table_loader[:], in_=ones[:], func=ACT.Abs_reciprocal_sqrt, bias=0.0, scale=1.0
        )

        def warm(bank, times):
            for i in range(times):
                nc.tensor.matmul(out=bank, lhsT=zeros[:], rhs=zeros[:], start=True, stop=True)

        packed = {}

        def flip(rows, grouped, is_weight, engine, pool, dummies=0):
            tiles = rows.shape[1] // WIDTH
            flipped = pool.tile([P, tiles, 2, P], F32, tag="bank")
            warm(flipped[:, 0, 0, :], dummies)
            words = rows.bitcast(F32).rearrange("p (a l r) -> p a l r", a=tiles, l=2)
            for a in range(tiles):
                for l in range(2):
                    nc.tensor.transpose(flipped[:, a, l, :], words[:, a, l, :], ident_f32[:])
            target = grouped.bitcast(F32)
            if is_weight:
                source = flipped[:].rearrange("p a l r -> p r a l")
                target = target.rearrange("p (r a l) -> p r a l", a=2, l=2)
            else:
                source = flipped[:].rearrange("p a l r -> p a r l")
                target = target.rearrange("p (a r l) -> p a r l", a=tiles, l=2)
            if engine == "scalar":
                nc.scalar.copy(out=target, in_=source)
            else:
                nc.vector.tensor_copy(out=target, in_=source)

        grouped_of = {}

        def flip_rows(name, engine, pool=banks, dummies=0):
            grouped = grouped_pool.tile([P, PAIR * PACK], BF16, name="grouped_" + name, align_bytes=64)
            flip(raw_of[name], grouped[:], name[0] == "W", engine, pool, dummies)
            grouped_of[name] = grouped

        def quantise(name):
            columns = grouped_of[name].shape[1] // PACK
            codes = operands.tile([P, columns], U32, name=name + "_codes", align_bytes=64)
            scales = operands.tile([P, columns], U8, name=name + "_scales", align_bytes=64)
            nc.vector.quantize_mx(
                out=codes[:].bitcast(FP8X4), scales=scales[:], in_=grouped_of[name][:]
            )
            packed[name] = (codes, scales)

        terms = {}

        def add_bias_relu(engine, target, source, i_bias, column):
            bias = bias_cols[i_bias][:, column : column + 1]
            if engine == "scalar":
                nc.scalar.activation(out=target, in_=source, func=ACT.Relu, bias=bias, scale=1.0)
            else:
                nc.vector.tensor_scalar(
                    out=target, in0=source, scalar1=bias, scalar2=0.0, op0=ALU.add, op1=ALU.max
                )

        sources = {
            "r0": ("W0", "q", (0, 0)), "r1": ("W1", "h", (0, 1)), "y": ("W2", "h", (0, 2)),
            "r3": ("W3", "q", (1, 0)), "c": ("Wc", "ge", (1, 1)),
        }

        def relu_tile(name, t, engines=("scalar",)):
            weight, tokens, (i_bias, j) = sources[name]
            pair, a = divmod(t, 2)
            if name == "c":
                t_codes, t_scales = packed["ge_%d" % t]
                columns = slice(0, P)
            else:
                t_codes, t_scales = packed["%s_%d" % (tokens, pair)]
                columns = slice(a * P, (a + 1) * P)
            if a == 0:
                terms[name, pair] = major.tile([P, TILES, PAIR], F32, name=name, bufs=4)
            share = TILES // len(engines)
            for i, engine in enumerate(engines):
                acc = banks.tile([P, share, P], F32, tag="bank")
                for k in range(share):
                    f = i * share + k
                    w_codes, w_scales = packed["%s_%d" % (weight, f // 2)]
                    features = slice((f % 2) * P, (f % 2 + 1) * P)
                    nc.tensor.matmul_mx(
                        out=acc[:, k, :],
                        lhsT=w_codes[:, features].bitcast(FP8X4),
                        lhsT_scale=w_scales[:, features],
                        rhs=t_codes[:, columns].bitcast(FP8X4),
                        rhs_scale=t_scales[:, columns],
                        start=True,
                        stop=True,
                    )
                for k in range(share):
                    f = i * share + k
                    target = terms[name, pair][:, f, a * P : (a + 1) * P]
                    add_bias_relu(engine, target, acc[:, k, :], i_bias, j * TILES + f)

        def relu_half(name, pair, half, engine):
            weight, tokens, (i_bias, j) = sources[name]
            w_codes, w_scales = packed["%s_%d" % (weight, half)]
            t_codes, t_scales = packed["%s_%d" % (tokens, pair)]
            if half == 0:
                terms[name, pair] = major.tile([P, TILES, PAIR], F32, name=name, bufs=4)
            result = terms[name, pair]
            acc = banks.tile([P, 2, PAIR], F32, tag="bank")
            for i in range(2):
                features = slice(i * P, (i + 1) * P)
                nc.tensor.matmul_mx(
                    out=acc[:, i, :],
                    lhsT=w_codes[:, features].bitcast(FP8X4),
                    lhsT_scale=w_scales[:, features],
                    rhs=t_codes[:].bitcast(FP8X4),
                    rhs_scale=t_scales[:],
                    start=True,
                    stop=True,
                )
            for i in range(2):
                f = 2 * half + i
                add_bias_relu(engine, result[:, f, :], acc[:, i, :], i_bias, j * TILES + f)

        def relu_term(name, pair):
            for half in range(2):
                relu_half(name, pair, half, "scalar")

        def turn_sum(bank, parts, a, features=range(TILES)):
            for k, f in enumerate(features):
                for i, part in enumerate(parts):
                    nc.tensor.matmul(
                        out=bank[:, k * P : (k + 1) * P],
                        lhsT=part[:, f, a * P : (a + 1) * P],
                        rhs=ident_f32[:],
                        is_transpose=True,
                        start=(i == 0),
                        stop=(i == len(parts) - 1),
                    )

        turned = {}
        moments = {}
        inverse = {}
        centred = {}
        normed = {}
        ge_of = {}

        def turn_tile(t):
            pair, a = divmod(t, 2)
            x_bank = norm_banks.tile([P, WIDTH], F32, tag="bank")
            turn_sum(x_bank, [terms["r0", pair], terms["r1", pair]], a)
            y_bank = norm_banks.tile([P, WIDTH], F32, tag="bank")
            turn_sum(y_bank, [terms["y", pair]], a)
            turned[t] = (x_bank, y_bank)

        def statistics(t, i, stats):
            nc.vector.bn_stats(out=stats[:, i, :], in_=turned[t][i][:])

        def centre(t, i, mean_var):
            result = work.tile([P, WIDTH], F32, name="centred%d" % i)
            nc.vector.scalar_tensor_tensor(
                out=result[:], in0=turned[t][i][:], scalar=mean_var[:, i, 0:1],
                in1=repeated[:, i, :], op0=ALU.subtract, op1=ALU.mult,
            )
            return result

        def shift(t, i):
            source, inv_std = centred[t][i], inverse[t]
            result = work.tile([P, WIDTH], F32, name="normed%d" % i)
            nc.vector.scalar_tensor_tensor(
                out=result[:], in0=source[:], scalar=inv_std[:, i : i + 1],
                in1=repeated[:, 2 + i, :], op0=ALU.mult, op1=ALU.add,
            )
            normed[t, i] = result

        def gate(t):
            pair, a = divmod(t, 2)
            if a == 0:
                ge_of[pair] = work.tile([P, 2 * WIDTH], BF16, name="ge_rows")
            engine = nc.vector if t >= 2 * PAIRS - 2 else nc.gpsimd
            engine.tensor_tensor(
                out=ge_of[pair][:, a * WIDTH : (a + 1) * WIDTH],
                in0=normed[t, 0][:], in1=normed[t, 1][:], op=ALU.mult,
            )

        def norms(t, middle=(), late=()):
            now, before = t < 2 * PAIRS, t > 0
            if now:
                stats = small.tile([P, 2, 6], F32)
                mean_var = small.tile([P, 2, 2], F32)
                moments[t] = mean_var
                statistics(t, 0, stats)
            if before:
                shift(t - 1, 0)
            if now:
                statistics(t, 1, stats)
                nc.vector.bn_aggr(out=mean_var[:, 0, :], in_=stats[:, 0, :])
            if before:
                shift(t - 1, 1)
            if now:
                nc.vector.bn_aggr(out=mean_var[:, 1, :], in_=stats[:, 1, :])
            for name in middle:
                quantise(name)
            if now:
                x = centre(t, 0, mean_var)
            if before:
                gate(t - 1)
            if now:
                y = centre(t, 1, mean_var)
                centred[t] = (x, y)
            for name in late:
                quantise(name)

        def invert(t):
            inv_std = small.tile([P, 2], F32)
            nc.scalar.activation(
                out=inv_std[:], in_=moments[t][:, :, 1], func=ACT.Abs_reciprocal_sqrt,
                bias=EPS, scale=1.0,
            )
            inverse[t] = inv_std

        def flip_gate(pair, a, tiles, engine="scalar"):
            name = "ge_%d" % (pair if tiles == 2 else 2 * pair + a)
            grouped = work.tile([P, tiles * P * PACK], BF16, name="ge_grouped%d" % tiles, align_bytes=64)
            rows = ge_of[pair][:, a * WIDTH : (a + tiles) * WIDTH]
            flip(rows, grouped[:], False, engine, banks, 2 if pair == PAIRS - 1 and a == 1 else 0)
            grouped_of[name] = grouped

        def store_tile(pair, a, engines=("scalar",), on_gpsimd=False):
            parts, tile = [terms["r3", pair], terms["c", pair]], a
            if on_gpsimd:
                total = work.tile([P, TILES, P], F32, name="total")
                cols = slice(a * P, (a + 1) * P)
                nc.gpsimd.tensor_tensor(
                    out=total[:], in0=parts[0][:, :, cols], in1=parts[1][:, :, cols], op=ALU.add
                )
                parts, tile = [total], 0
            share = TILES // len(engines)
            width = share * P
            for i, engine in enumerate(engines):
                bank = banks.tile([P, width], F32, tag="bank")
                turn_sum(bank, parts, tile, range(i * share, (i + 1) * share))
                result = work.tile([P, width], F32, name="result%d" % width, bufs=4)
                if engine == "scalar":
                    nc.scalar.copy(out=result[:], in_=bank[:])
                else:
                    nc.vector.tensor_copy(out=result[:], in_=bank[:])
                cols = slice(i * width, (i + 1) * width)
                nc.sync.dma_start(out=out_view[:, 2 * pair + a, cols], in_=result[:])

        repeated = const.tile([P, 4, WIDTH], BF16)
        spread = {}

        def repeat_rows(half, pool):
            spread[half] = pool.tile([P, 2, WIDTH], BF16, tag="bank", name="spread")
            for i in range(2):
                j = 2 * half + i
                nc.tensor.matmul(
                    out=spread[half][:, i, :],
                    lhsT=ident_bf16[:, j : j + 1].to_broadcast([P, P]),
                    rhs=norm_rows[:],
                    start=True,
                    stop=True,
                )

        def copy_repeated(half, engine):
            target = repeated[:, 2 * half : 2 * half + 2, :]
            if engine == "scalar":
                nc.scalar.copy(out=target, in_=spread[half][:])
            else:
                nc.vector.tensor_copy(out=target, in_=spread[half][:])

        bias_cols = []

        def flip_bias(i, engine):
            bias_flipped = banks.tile([P, P], BF16, tag="bank")
            nc.tensor.transpose(bias_flipped[:], bias_rows[i][:], ident_bf16[:])
            cols = const.tile([P, P], F32, name="bias_cols%d" % i)
            if engine == "scalar":
                nc.scalar.copy(out=cols[:], in_=bias_flipped[:])
            else:
                nc.vector.tensor_copy(out=cols[:], in_=bias_flipped[:])
            bias_cols.append(cols)

        flip_rows("q_0", "vector", dummies=5)
        flip_rows("W0_0", "scalar")
        quantise("q_0")
        flip_rows("W0_1", "vector")
        quantise("W0_0")
        quantise("W0_1")
        flip_rows("h_0", "scalar")
        flip_rows("W1_0", "vector", norm_banks, dummies=2)
        quantise("h_0")
        flip_rows("W1_1", "scalar", norm_banks)
        quantise("W1_0")
        flip_bias(0, "vector")
        relu_half("r0", 0, 0, "scalar")
        flip_rows("W2_0", "vector", norm_banks)
        quantise("W1_1")
        flip_rows("W2_1", "scalar", norm_banks)
        quantise("W2_0")
        relu_half("r0", 0, 1, "scalar")
        relu_half("r1", 0, 0, "scalar")
        quantise("W2_1")
        relu_half("r1", 0, 1, "vector")
        relu_half("y", 0, 0, "scalar")
        relu_half("y", 0, 1, "vector")
        repeat_rows(0, norm_banks)
        turn_tile(0)
        copy_repeated(0, "scalar")
        flip_rows("q_1", "scalar")
        flip_rows("h_1", "scalar")
        repeat_rows(1, banks)
        copy_repeated(1, "scalar")
        turn_tile(1)

        norms(0, middle=("q_1", "h_1"))
        invert(0)
        relu_term("r0", 1)
        relu_term("r1", 1)

        flip_rows("q_2", "scalar")
        flip_rows("h_2", "scalar")
        norms(1, late=("q_2", "h_2"))
        relu_term("y", 1)
        invert(1)
        flip_bias(1, "scalar")
        turn_tile(2)
        relu_term("r0", 2)

        flip_rows("W3_0", "scalar")
        flip_rows("W3_1", "scalar")
        norms(2, late=("W3_0", "W3_1"))
        relu_term("r1", 2)
        invert(2)
        turn_tile(3)
        relu_term("y", 2)

        flip_gate(0, 0, 2)
        flip_rows("q_3", "scalar")
        flip_rows("h_3", "scalar")
        norms(3, late=("q_3", "h_3", "ge_0"))
        relu_term("r3", 0)
        invert(3)
        turn_tile(4)
        flip_rows("Wc_0", "scalar")
        flip_rows("Wc_1", "scalar")

        norms(4, late=("Wc_0", "Wc_1"))
        relu_term("r0", 3)
        turn_tile(5)
        relu_term("r1", 3)
        invert(4)
        relu_term("r3", 1)

        flip_gate(1, 0, 2)
        norms(5, late=("ge_1",))
        relu_term("y", 3)
        relu_term("c", 0)
        invert(5)
        turn_tile(6)
        relu_term("r3", 2)

        store_tile(0, 0)
        norms(6)
        turn_tile(7)
        relu_term("c", 1)
        invert(6)
        store_tile(0, 1)
        relu_term("r3", 3)

        flip_gate(2, 0, 2)
        store_tile(1, 0)
        norms(7, middle=("ge_2",))
        store_tile(1, 1)
        invert(7)
        relu_term("c", 2)

        s = PAIRS - 1
        flip_gate(s, 0, 1)
        shift(2 * s + 1, 0)
        shift(2 * s + 1, 1)
        gate(2 * s + 1)
        store_tile(s - 1, 0)
        quantise("ge_%d" % (2 * s))
        flip_gate(s, 1, 1, "vector")
        quantise("ge_%d" % (2 * s + 1))
        relu_tile("c", 2 * s)
        store_tile(s - 1, 1)
        relu_tile("c", 2 * s + 1, ("scalar", "vector"))
        store_tile(s, 0)
        store_tile(s, 1, ("scalar", "vector"))
